import numpy as np
import ml_dtypes


def mxq(x, axis, fmt="e4m3"):
    dtype, down = {"e4m3": (ml_dtypes.float8_e4m3fn, 7), "e5m2": (ml_dtypes.float8_e5m2, 14)}[fmt]
    v = np.moveaxis(np.asarray(x, np.float32).astype(ml_dtypes.bfloat16).astype(np.float64), axis, -1)
    blocks = v.reshape(v.shape[:-1] + (-1, 32))
    amax = np.abs(blocks).max(-1, keepdims=True)
    byte = np.maximum(np.where(amax > 0, np.frexp(amax)[1] - 1 + 127, 0) - down, 1)
    scale = np.exp2(byte - 127.0)
    codes = (blocks / scale).astype(np.float32).astype(dtype).astype(np.float64)
    return np.moveaxis((codes * scale).reshape(v.shape), -1, axis)


WIDE = False


def mx_kscale(k):
    if not WIDE:
        return np.ones(k)
    levels = np.array([10, -10, 5, -5, 0])
    a = np.random.permutation(np.resize(levels, k // 512 * 4)).reshape(k // 512, 4)
    idx = np.arange(k)
    return np.exp2(a[idx // 512, idx % 128 // 32])


BF16 = ml_dtypes.bfloat16


def bf(x):
    return np.asarray(x, np.float32).astype(BF16)


def f64(x):
    return np.asarray(x).astype(np.float64)


E2M1 = np.array([0.0, 0.5, 1.0, 1.5, 2.0, 3.0, 4.0, 6.0, -0.0, -0.5, -1.0, -1.5, -2.0, -3.0, -4.0, -6.0])


def pack_weight(w, fmt):
    k, n = w.shape
    w = f64(bf(w)).reshape(k // 32, 32, n)
    amax = np.abs(w).max(1)
    if fmt == "e4m3":
        byte = np.frexp(amax)[1] - 1 + 127 - 7
    else:
        mant, ex = np.frexp(amax / 6.0)
        byte = np.where(mant > 0.5, ex, ex - 1) + 127
    byte = np.clip(np.where(amax > 0, byte, 1), 1, 254)
    scaled = (w * np.exp2(127.0 - byte)[:, None, :]).reshape(k, n).astype(np.float32)
    by_word = np.ascontiguousarray(scaled.reshape(k // 512, 128, 4, n).transpose(0, 1, 3, 2))
    if fmt == "e4m3":
        words = by_word.astype(ml_dtypes.float8_e4m3fn).view(np.uint8)
    else:
        c = by_word.astype(ml_dtypes.float4_e2m1fn).view(np.uint8) & 0xF
        words = c[..., 0::2] | (c[..., 1::2] << 4)
    return np.ascontiguousarray(words), np.ascontiguousarray(byte.astype(np.uint8).reshape(k // 512, 16, n))


def unpack_weight(words, scales, fmt):
    g, p, n, _ = words.shape
    if fmt == "e4m3":
        vals = np.ascontiguousarray(words).view(ml_dtypes.float8_e4m3fn).astype(np.float64)
    else:
        nib = np.empty((g, p, n, 4), np.uint8)
        nib[..., 0::2] = words & 0xF
        nib[..., 1::2] = words >> 4
        vals = E2M1[nib]
    vals = vals * np.repeat(np.exp2(scales.astype(np.float64) - 127.0), 8, axis=1)[..., None]
    return vals.transpose(0, 1, 3, 2).reshape(g * 512, n)


B, F, C, DEPTH, LQ = 2048, 1024, 1024, 11, 7
NL = 2 ** (DEPTH - 1)
NQ = 2 ** LQ


def sigmoid(v):
    return 1.0 / (1.0 + np.exp(-v))


def setup_inputs():
    s = mx_kscale(F)
    x = bf(np.random.standard_normal((B, F)) * s)
    W_gate = bf(np.random.standard_normal((F, NL - 1)) * 2.0 / np.sqrt(F) / s[:, None])
    b_gate = bf(np.random.standard_normal(NL - 1) * 0.5)
    words, scales = pack_weight(np.random.standard_normal((NL, C)) * 0.5 * 1.2 ** (DEPTH - 1), "e4m3")
    return {"x": x,
            "W_gate": W_gate,
            "b_gate": b_gate,
            "leaf_logits_words": words,
            "leaf_logits_scales": scales}


def reference(x, W_gate, b_gate, leaf_logits_words, leaf_logits_scales):
    nb = x.shape[0]
    xf, wf = f64(x), f64(W_gate)
    top = (xf @ wf[:, :NQ])[:, :NQ - 1]
    low = mxq(xf, 1, "e4m3") @ mxq(wf[:, NQ - 1:], 0, "e4m3")
    p = sigmoid(np.concatenate([top, low], axis=1) + f64(b_gate))
    probs = np.ones((nb, 1))
    for level in range(DEPTH - 1):
        n = 2 ** level
        start = n - 1
        pl = p[:, start:start + n]
        probs = np.stack([(1.0 - pl) * probs, pl * probs], axis=-1).reshape(nb, 2 * n)
    return mxq(probs, 1, "e4m3") @ unpack_weight(leaf_logits_words, leaf_logits_scales, "e4m3")

@@ -1,0 +1,358 @@
+from contextlib import ExitStack
+
+import concourse.mybir as mybir
+from concourse.masks import make_identity
+
+F32 = mybir.dt.float32
+BF16 = mybir.dt.bfloat16
+I32 = mybir.dt.int32
+U32 = mybir.dt.uint32
+U8 = mybir.dt.uint8
+FP8X4 = mybir.dt.float8_e4m3fn_x4
+ALU = mybir.AluOpType
+SIGMOID = mybir.ActivationFunctionType.Sigmoid
+
+P = 128
+BATCH = 2048
+FEATURES = 1024
+CLASSES = 1024
+PASSES = 2
+CHUNK = 512
+HALF = CHUNK // 2
+ROW_TILES = CHUNK // P
+CHUNKS = BATCH // CHUNK
+TOP = 128
+SLOTS = 8
+
+FLOPS = 2 * BATCH * FEATURES * (TOP + 896) + 2 * BATCH * 1024 * CLASSES
+
+
+def tile_treemodel_kernel(tc, x, W_gate, b_gate, leaf_logits_words, leaf_logits_scales, out):
+    nc = tc.nc
+    with ExitStack() as ctx:
+        const = ctx.enter_context(tc.tile_pool(name="const", bufs=1))
+        xin = ctx.enter_context(tc.tile_pool(name="xin", bufs=CHUNKS))
+        work = ctx.enter_context(tc.tile_pool(name="work", bufs=2))
+        ostage = ctx.enter_context(tc.tile_pool(name="ostage", bufs=4))
+        psum_stream = ctx.enter_context(tc.psum_pool(name="psum_stream", bufs=3))
+        psum_top = ctx.enter_context(tc.psum_pool(name="psum_top", bufs=1))
+        psum_pt = ctx.enter_context(tc.psum_pool(name="psum_pt", bufs=2))
+        psum_o = ctx.enter_context(tc.psum_pool(name="psum_o", bufs=2))
+        ctx.enter_context(tc.manual_schedule())
+
+        x_chunks = x.rearrange("(n p q) k -> n p q k", p=P, q=ROW_TILES)
+        out_tiles = out.rearrange("(n p q) c -> n q p c", p=P, q=ROW_TILES)
+
+        bias_row = const.tile([P, TOP], BF16)
+        nc.vector.memset(bias_row[:], 0.0)
+        b_src = const.tile([P, 256], BF16)
+        nc.vector.memset(b_src[:], 0.0)
+        nc.scalar.dma_start(out=bias_row[0:1, :], in_=b_gate[0:TOP].rearrange("(o m) -> o m", o=1))
+        level9_bias = b_gate[511:1023].rearrange("(g m) -> g m", g=2)
+        for c in range(2):
+            nc.scalar.dma_start(out=b_src[2 * c : 2 * c + 2, 0:255], in_=level9_bias[:, c : c + 255])
+        nc.scalar.dma_start(out=b_src[32:34, 0:128], in_=b_gate[255:511].rearrange("(g m) -> g m", g=2))
+        nc.scalar.dma_start(out=b_src[64:66, 0:64], in_=b_gate[127:255].rearrange("(g j) -> g j", g=2))
+
+        x_rows = []
+        for n in range(CHUNKS):
+            x_rows.append(xin.tile([P, ROW_TILES, FEATURES], BF16, name="x_sb"))
+        w_raw = const.tile([P, 4, 2, 1024], BF16)
+        w_rows = W_gate.rearrange("(a p e) c -> a p e c", a=4, p=P, e=2)
+        nc.sync.dma_start(out=x_rows[0][:], in_=x_chunks[0])
+        for a in range(4):
+            nc.sync.dma_start(out=w_raw[:, a, :, 0:1023], in_=w_rows[a])
+        w_planes = w_raw[:].rearrange("p (g u) e c -> p g (u e) c", g=PASSES)
+        for n in range(1, CHUNKS):
+            nc.sync.dma_start(out=x_rows[n][:], in_=x_chunks[n])
+
+        leaf_scales = const.tile([P, PASSES, CLASSES], U8, align_bytes=64)
+        nc.vector.memset(leaf_scales[:].rearrange("p g n -> p (g n)").bitcast(I32), 0)
+        scale_rows = leaf_logits_scales.rearrange("g (k r) n -> r k g n", r=4)
+        for r in range(4):
+            nc.sync.dma_start(out=leaf_scales[r:P:32, :, :].bitcast(I32), in_=scale_rows[r].bitcast(I32))
+        leaf_words = const.tile([P, PASSES, 4 * CLASSES], U8, align_bytes=64)
+        for g in range(PASSES):
+            nc.sync.dma_start(
+                out=leaf_words[:, g, :].bitcast(I32),
+                in_=leaf_logits_words[g].rearrange("p n t -> p (n t)").bitcast(I32),
+            )
+
+        ident = const.tile([P, P], F32)
+        make_identity(nc, ident[:])
+        ones = const.tile([P, P], BF16)
+        nc.vector.memset(ones[:], 1.0)
+        warm_in = const.tile([P, 1], F32)
+        warm_out = const.tile([P, 1], F32)
+        nc.vector.memset(warm_in[:], 0.0)
+        nc.scalar.activation(out=warm_out[:], in_=warm_in[:], func=SIGMOID)
+
+        b_all = const.tile([P, P], F32)
+        nc.vector.tensor_copy(out=b_all[0:32, :], in_=b_src[0:32, 0:256:2])
+        nc.vector.tensor_copy(out=b_all[32:64, :], in_=b_src[32:64, 0:128])
+        b_pairs = b_all[:].rearrange("p (j d) -> p j d", d=2)
+        nc.vector.tensor_copy(out=b_pairs[64:96, :, 1], in_=b_src[64:96, 0:64])
+        nc.vector.tensor_scalar_mul(out=b_pairs[64:96, :, 0], in0=b_src[64:96, 0:64], scalar1=-1.0)
+        nc.vector.memset(b_pairs[96:128, :, 1], 1.0)
+        nc.vector.memset(b_pairs[96:128, :, 0], -1.0)
+        bias_cols = const.tile([P, P], F32)
+
+        def spread_bias():
+            b_ps = psum_pt.tile([P, P], F32, name="pt")
+            nc.tensor.transpose(out=b_ps[:], in_=b_all[:], identity=ident[:])
+            nc.vector.tensor_copy(out=bias_cols[:], in_=b_ps[:])
+
+        def column(i):
+            return bias_cols[:, i : i + 1]
+
+        wg = const.tile([P, PASSES, SLOTS * P, 4], BF16, align_bytes=64)
+        wc = const.tile([P, PASSES, SLOTS * P], U32, align_bytes=64)
+        ws = const.tile([P, PASSES, SLOTS * P], U8, align_bytes=64)
+
+        def regroup_levels_7_8(g):
+            nc.vector.tensor_copy(
+                out=wg[:, g, 0:256, :].rearrange("p (j d) t -> p j d t", d=2),
+                in_=w_planes[:, g, :, 127:255].rearrange("p t j -> p j t").unsqueeze(2).to_broadcast([P, 128, 2, 4]),
+            )
+            nc.vector.tensor_copy(
+                out=wg[:, g, 256:512, :],
+                in_=w_planes[:, g, :, 255:511].rearrange("p t j -> p j t"),
+            )
+
+        def regroup_level_9(g):
+            nc.vector.tensor_copy(
+                out=wg[:, g, 512:1024, :].rearrange("p (c j) t -> p c j t", c=2),
+                in_=w_planes[:, g, :, 511:1023].rearrange("p t (j c) -> p c j t", c=2),
+            )
+
+        def quantise_w(g, first):
+            nc.vector.quantize_mx(
+                out=wc[:, g, first : first + 512].bitcast(FP8X4),
+                scales=ws[:, g, first : first + 512],
+                in_=wg[:, g, first : first + 512, :].rearrange("p n t -> p (n t)"),
+            )
+
+        xg_of = {}
+        xq_of = {}
+
+        def x_transpose(n):
+            x_sb = x_rows[n]
+            xg = work.tile([P, PASSES, CHUNK, 4], BF16, align_bytes=64)
+            for g in range(PASSES):
+                for h in range(2):
+                    xt = psum_stream.tile([P, 2, HALF], F32, name="stream")
+                    for u in range(2):
+                        for qq in range(2):
+                            words = x_sb[:, 2 * h + qq, :].bitcast(F32)
+                            first = 256 * g + 128 * u
+                            nc.tensor.transpose(
+                                out=xt[:, u, P * qq : P * qq + P],
+                                in_=words[:, first : first + P],
+                                identity=ident[:],
+                            )
+                    dst = xg[:, g, HALF * h : HALF * h + HALF, :].rearrange("p b t -> p (b t)").bitcast(F32)
+                    nc.scalar.copy(
+                        out=dst.rearrange("p (b u) -> p b u", u=2),
+                        in_=xt[:].rearrange("p u b -> p b u"),
+                    )
+            xg_of[n] = xg
+
+        def x_quantise(n):
+            xg = xg_of[n]
+            xc = work.tile([P, PASSES, CHUNK], U32, align_bytes=64)
+            xs = work.tile([P, PASSES, CHUNK], U8, align_bytes=64)
+            for g in range(PASSES):
+                nc.vector.quantize_mx(
+                    out=xc[:, g, :].bitcast(FP8X4),
+                    scales=xs[:, g, :],
+                    in_=xg[:, g].rearrange("p b t -> p (b t)"),
+                )
+            xq_of[n] = (xc, xs)
+
+        turn_of = {}
+        reach7_of = {}
+
+        def top_logits(n):
+            xg = xg_of[n]
+            top = psum_top.tile([P, ROW_TILES, TOP], F32)
+            for q in range(ROW_TILES):
+                for g in range(PASSES):
+                    for t in range(4):
+                        nc.tensor.matmul(
+                            out=top[:, q, :],
+                            lhsT=xg[:, g, P * q : P * q + P, t],
+                            rhs=w_planes[:, g, t, 0:TOP],
+                            start=(g == 0 and t == 0),
+                            stop=False,
+                        )
+                nc.tensor.matmul(out=top[:, q, :], lhsT=ones[:], rhs=bias_row[:], start=False, stop=True)
+            turn = work.tile([P, 2, ROW_TILES, TOP], F32)
+            nc.scalar.activation(out=turn[:, 1], in_=top[:], func=SIGMOID)
+            nc.scalar.activation(out=turn[:, 0], in_=top[:], func=SIGMOID, scale=-1.0)
+            turn_of[n] = turn
+
+        def top_sweep(n):
+            turn = turn_of[n]
+            reach = turn[:, :, :, 0].rearrange("p j q -> p q j")
+            for level in range(1, 6):
+                nodes = 2**level
+                children = work.tile([P, ROW_TILES, 2 * nodes], F32, name="reach%d" % (level + 1))
+                nc.vector.tensor_tensor(
+                    out=children[:].rearrange("p q (j c) -> p q j c", c=2),
+                    in0=reach.unsqueeze(3).to_broadcast([P, ROW_TILES, nodes, 2]),
+                    in1=turn[:, :, :, nodes - 1 : 2 * nodes - 1].rearrange("p c q j -> p q j c"),
+                    op=ALU.mult,
+                )
+                reach = children[:]
+            reach7 = work.tile([P, ROW_TILES, 256], F32)
+            for q in range(ROW_TILES):
+                nc.vector.tensor_tensor(
+                    out=reach7[:, q, :].rearrange("p (j c d) -> p j c d", c=2, d=2),
+                    in0=reach[:, q, :].unsqueeze(2).unsqueeze(3).to_broadcast([P, 64, 2, 2]),
+                    in1=turn[:, :, q, 63:127].rearrange("p c j -> p j c").unsqueeze(3).to_broadcast([P, 64, 2, 2]),
+                    op=ALU.mult,
+                )
+            reach7_of[n] = reach7
+
+        low_of = {}
+        pt_of = {}
+
+        def low_logits(xc, xs, slot):
+            z = psum_stream.tile([P, CHUNK], F32, name="stream")
+            for g in range(PASSES):
+                nc.tensor.matmul_mx(
+                    out=z[:],
+                    lhsT=wc[:, g, P * slot : P * slot + P].bitcast(FP8X4),
+                    lhsT_scale=ws[:, g, P * slot : P * slot + P],
+                    rhs=xc[:, g, :].bitcast(FP8X4),
+                    rhs_scale=xs[:, g, :],
+                    start=(g == 0),
+                    stop=(g == PASSES - 1),
+                )
+            return z
+
+        def low_turns(n):
+            xc, xs = xq_of[n]
+            turn7 = work.tile([P, 2, CHUNK], F32)
+            right8 = work.tile([P, 2, CHUNK], F32)
+            right9 = work.tile([P, 2, 2, CHUNK], F32)
+            for g in range(2):
+                z = low_logits(xc, xs, g)
+                nc.scalar.activation(out=turn7[:, g, :], in_=z[:], func=SIGMOID, bias=column(64 + g), scale=column(96))
+            for g in range(2):
+                z = low_logits(xc, xs, 2 + g)
+                nc.scalar.activation(out=right8[:, g, :], in_=z[:], func=SIGMOID, bias=column(32 + g))
+            for c in range(2):
+                for g in range(2):
+                    z = low_logits(xc, xs, 4 + 2 * c + g)
+                    nc.scalar.activation(out=right9[:, g, c, :], in_=z[:], func=SIGMOID, bias=column(2 * c + g))
+            low_of[n] = (turn7, right8, right9)
+
+        def reach7_transpose(n):
+            reach7 = reach7_of[n]
+            banks = []
+            for g in range(2):
+                pt = psum_pt.tile([P, CHUNK], F32)
+                for q in range(ROW_TILES):
+                    nc.tensor.transpose(
+                        out=pt[:, P * q : P * q + P],
+                        in_=reach7[:, q, P * g : P * g + P],
+                        identity=ident[:],
+                    )
+                banks.append(pt)
+            pt_of[n] = banks
+
+        minus9_of = {}
+
+        def reach_8_9(n):
+            turn7, right8, right9 = low_of[n]
+            minus8 = work.tile([P, 2, CHUNK], F32)
+            for g in range(2):
+                nc.vector.scalar_tensor_tensor(
+                    out=minus8[:, g, :], in0=pt_of[n][g][:], scalar=-1.0, in1=turn7[:, g, :], op0=ALU.mult, op1=ALU.mult
+                )
+            minus9 = work.tile([P, 2, 2, CHUNK], F32)
+            nc.vector.tensor_tensor(out=minus9[:, :, 1, :], in0=minus8[:], in1=right8[:], op=ALU.mult)
+            nc.vector.tensor_tensor(out=minus9[:, :, 0, :], in0=minus8[:], in1=minus9[:, :, 1, :], op=ALU.subtract)
+            minus9_of[n] = minus9
+
+        pq_of = {}
+
+        def leaf_probs(n):
+            right9 = low_of[n][2]
+            minus9 = minus9_of[n]
+            probs = work.tile([P, PASSES, CHUNK, 4], BF16, align_bytes=64)
+            pc = work.tile([P, PASSES, CHUNK], U32, align_bytes=64)
+            ps = work.tile([P, PASSES, CHUNK], U8, align_bytes=64)
+            for h in range(2):
+                cols = slice(HALF * h, HALF * h + HALF)
+                for g in range(PASSES):
+                    pairs = probs[:, g, cols, :].rearrange("p b (c e) -> p b c e", e=2)
+                    turn_right = right9[:, g, :, cols].rearrange("p c b -> p b c")
+                    parent = minus9[:, g, :, cols].rearrange("p c b -> p b c")
+                    nc.vector.scalar_tensor_tensor(
+                        out=pairs[:, :, :, 1], in0=turn_right, scalar=-1.0, in1=parent, op0=ALU.mult, op1=ALU.mult
+                    )
+                    nc.vector.scalar_tensor_tensor(
+                        out=pairs[:, :, :, 0], in0=turn_right, scalar=1.0, in1=parent, op0=ALU.subtract, op1=ALU.mult
+                    )
+                for g in range(PASSES):
+                    nc.vector.quantize_mx(
+                        out=pc[:, g, cols].bitcast(FP8X4),
+                        scales=ps[:, g, cols],
+                        in_=probs[:, g, cols, :].rearrange("p b t -> p (b t)"),
+                    )
+            pq_of[n] = (pc, ps)
+
+        def leaves(n):
+            pc, ps = pq_of[n]
+            for q in range(ROW_TILES):
+                rows = ostage.tile([P, CLASSES], F32)
+                for half in range(2):
+                    acc = psum_o.tile([P, 512], F32)
+                    for g in range(PASSES):
+                        nc.tensor.matmul_mx(
+                            out=acc[:],
+                            lhsT=pc[:, g, P * q : P * q + P].bitcast(FP8X4),
+                            lhsT_scale=ps[:, g, P * q : P * q + P],
+                            rhs=leaf_words[:, g, 2048 * half : 2048 * half + 2048].bitcast(FP8X4),
+                            rhs_scale=leaf_scales[:, g, 512 * half : 512 * half + 512],
+                            start=(g == 0),
+                            stop=(g == PASSES - 1),
+                        )
+                    nc.scalar.copy(out=rows[:, 512 * half : 512 * half + 512], in_=acc[:])
+                nc.sync.dma_start(out=out_tiles[n, q], in_=rows[:])
+
+        def live(n):
+            return 0 <= n < CHUNKS
+
+        for n in range(-2, CHUNKS + 1):
+            if live(n):
+                reach_8_9(n)
+            if live(n - 1):
+                leaves(n - 1)
+            if live(n + 1):
+                top_sweep(n + 1)
+            if live(n + 2):
+                x_transpose(n + 2)
+            if n == -2:
+                spread_bias()
+                regroup_levels_7_8(0)
+            if n == -1:
+                for g in range(PASSES):
+                    regroup_level_9(g)
+                for g in range(PASSES):
+                    quantise_w(g, 512)
+            if live(n):
+                leaf_probs(n)
+            if live(n + 1):
+                low_turns(n + 1)
+                reach7_transpose(n + 1)
+            if live(n + 2):
+                x_quantise(n + 2)
+            if n == -2:
+                regroup_levels_7_8(1)
+                for g in range(PASSES):
+                    quantise_w(g, 0)
+            if live(n + 2):
+                top_logits(n + 2)

@@ -17,12 +17,14 @@ BATCH = 2048
 FEATURES = 1024
 CLASSES = 1024
 PASSES = 2
-CHUNK = 512
+CHUNK = 256
 HALF = CHUNK // 2
 ROW_TILES = CHUNK // P
 CHUNKS = BATCH // CHUNK
 TOP = 128
 SLOTS = 8
+SLOTS_PER_ROUND = SLOTS // ROW_TILES
+PLAIN_PASSES = 9
 
 FLOPS = 2 * BATCH * FEATURES * (TOP + 896) + 2 * BATCH * 1024 * CLASSES
 
@@ -35,13 +37,16 @@ def tile_treemodel_kernel(tc, x, W_gate, b_gate, leaf_logits_words, leaf_logits_
         work = ctx.enter_context(tc.tile_pool(name="work", bufs=2))
         ostage = ctx.enter_context(tc.tile_pool(name="ostage", bufs=4))
         psum_stream = ctx.enter_context(tc.psum_pool(name="psum_stream", bufs=3))
-        psum_top = ctx.enter_context(tc.psum_pool(name="psum_top", bufs=1))
-        psum_pt = ctx.enter_context(tc.psum_pool(name="psum_pt", bufs=2))
+        psum_top = ctx.enter_context(tc.psum_pool(name="psum_top", bufs=2))
+        psum_pt = ctx.enter_context(tc.psum_pool(name="psum_pt", bufs=1))
         psum_o = ctx.enter_context(tc.psum_pool(name="psum_o", bufs=2))
         ctx.enter_context(tc.manual_schedule())
 
         x_chunks = x.rearrange("(n p q) k -> n p q k", p=P, q=ROW_TILES)
         out_tiles = out.rearrange("(n p q) c -> n q p c", p=P, q=ROW_TILES)
+
+        def live(n):
+            return 0 <= n < CHUNKS
 
         bias_row = const.tile([P, TOP], BF16)
         nc.vector.memset(bias_row[:], 0.0)
@@ -120,7 +125,7 @@ def tile_treemodel_kernel(tc, x, W_gate, b_gate, leaf_logits_words, leaf_logits_
             )
 
         def regroup_level_9(g):
-            nc.vector.tensor_copy(
+            nc.scalar.copy(
                 out=wg[:, g, 512:1024, :].rearrange("p (c j) t -> p c j t", c=2),
                 in_=w_planes[:, g, :, 511:1023].rearrange("p t (j c) -> p c j t", c=2),
             )
@@ -137,58 +142,60 @@ def tile_treemodel_kernel(tc, x, W_gate, b_gate, leaf_logits_words, leaf_logits_
 
         def x_transpose(n):
             x_sb = x_rows[n]
-            xg = work.tile([P, PASSES, CHUNK, 4], BF16, align_bytes=64)
+            xg = work.tile([P, PASSES, CHUNK, 4], BF16, align_bytes=64, bufs=3)
             for g in range(PASSES):
-                for h in range(2):
-                    xt = psum_stream.tile([P, 2, HALF], F32, name="stream")
-                    for u in range(2):
-                        for qq in range(2):
-                            words = x_sb[:, 2 * h + qq, :].bitcast(F32)
-                            first = 256 * g + 128 * u
-                            nc.tensor.transpose(
-                                out=xt[:, u, P * qq : P * qq + P],
-                                in_=words[:, first : first + P],
-                                identity=ident[:],
-                            )
-                    dst = xg[:, g, HALF * h : HALF * h + HALF, :].rearrange("p b t -> p (b t)").bitcast(F32)
-                    nc.scalar.copy(
-                        out=dst.rearrange("p (b u) -> p b u", u=2),
-                        in_=xt[:].rearrange("p u b -> p b u"),
-                    )
+                xt = psum_stream.tile([P, 2, CHUNK], F32, name="stream")
+                for u in range(2):
+                    for q in range(ROW_TILES):
+                        first = 256 * g + 128 * u
+                        nc.tensor.transpose(
+                            out=xt[:, u, P * q : P * q + P],
+                            in_=x_sb[:, q, :].bitcast(F32)[:, first : first + P],
+                            identity=ident[:],
+                        )
+                nc.scalar.copy(
+                    out=xg[:, g].rearrange("p b t -> p (b t)").bitcast(F32).rearrange("p (b u) -> p b u", u=2),
+                    in_=xt[:].rearrange("p u b -> p b u"),
+                )
             xg_of[n] = xg
 
         def x_quantise(n):
-            xg = xg_of[n]
             xc = work.tile([P, PASSES, CHUNK], U32, align_bytes=64)
             xs = work.tile([P, PASSES, CHUNK], U8, align_bytes=64)
             for g in range(PASSES):
                 nc.vector.quantize_mx(
                     out=xc[:, g, :].bitcast(FP8X4),
                     scales=xs[:, g, :],
-                    in_=xg[:, g].rearrange("p b t -> p (b t)"),
+                    in_=xg_of[n][:, g].rearrange("p b t -> p (b t)"),
                 )
             xq_of[n] = (xc, xs)
 
+        top_of = {}
         turn_of = {}
         reach7_of = {}
 
-        def top_logits(n):
-            xg = xg_of[n]
-            top = psum_top.tile([P, ROW_TILES, TOP], F32)
-            for q in range(ROW_TILES):
-                for g in range(PASSES):
-                    for t in range(4):
-                        nc.tensor.matmul(
-                            out=top[:, q, :],
-                            lhsT=xg[:, g, P * q : P * q + P, t],
-                            rhs=w_planes[:, g, t, 0:TOP],
-                            start=(g == 0 and t == 0),
-                            stop=False,
-                        )
-                nc.tensor.matmul(out=top[:, q, :], lhsT=ones[:], rhs=bias_row[:], start=False, stop=True)
+        def top_open(n):
+            top_of[n] = psum_top.tile([P, ROW_TILES, TOP], F32, name="top")
+
+        def top_pass(n, q, k):
+            if not live(n) or k >= PLAIN_PASSES:
+                return
+            if k < PLAIN_PASSES - 1:
+                g, t = divmod(k, 4)
+                nc.tensor.matmul(
+                    out=top_of[n][:, q, :],
+                    lhsT=xg_of[n][:, g, P * q : P * q + P, t],
+                    rhs=w_planes[:, g, t, 0:TOP],
+                    start=(k == 0),
+                    stop=False,
+                )
+            else:
+                nc.tensor.matmul(out=top_of[n][:, q, :], lhsT=ones[:], rhs=bias_row[:], start=False, stop=True)
+
+        def top_turns(n):
             turn = work.tile([P, 2, ROW_TILES, TOP], F32)
-            nc.scalar.activation(out=turn[:, 1], in_=top[:], func=SIGMOID)
-            nc.scalar.activation(out=turn[:, 0], in_=top[:], func=SIGMOID, scale=-1.0)
+            nc.scalar.activation(out=turn[:, 1], in_=top_of[n][:], func=SIGMOID)
+            nc.scalar.activation(out=turn[:, 0], in_=top_of[n][:], func=SIGMOID, scale=-1.0)
             turn_of[n] = turn
 
         def top_sweep(n):
@@ -216,101 +223,100 @@ def tile_treemodel_kernel(tc, x, W_gate, b_gate, leaf_logits_words, leaf_logits_
 
         low_of = {}
         pt_of = {}
-
-        def low_logits(xc, xs, slot):
-            z = psum_stream.tile([P, CHUNK], F32, name="stream")
-            for g in range(PASSES):
-                nc.tensor.matmul_mx(
-                    out=z[:],
-                    lhsT=wc[:, g, P * slot : P * slot + P].bitcast(FP8X4),
-                    lhsT_scale=ws[:, g, P * slot : P * slot + P],
-                    rhs=xc[:, g, :].bitcast(FP8X4),
-                    rhs_scale=xs[:, g, :],
-                    start=(g == 0),
-                    stop=(g == PASSES - 1),
-                )
-            return z
-
-        def low_turns(n):
-            xc, xs = xq_of[n]
-            turn7 = work.tile([P, 2, CHUNK], F32)
-            right8 = work.tile([P, 2, CHUNK], F32)
-            right9 = work.tile([P, 2, 2, CHUNK], F32)
-            for g in range(2):
-                z = low_logits(xc, xs, g)
-                nc.scalar.activation(out=turn7[:, g, :], in_=z[:], func=SIGMOID, bias=column(64 + g), scale=column(96))
-            for g in range(2):
-                z = low_logits(xc, xs, 2 + g)
-                nc.scalar.activation(out=right8[:, g, :], in_=z[:], func=SIGMOID, bias=column(32 + g))
-            for c in range(2):
-                for g in range(2):
-                    z = low_logits(xc, xs, 4 + 2 * c + g)
-                    nc.scalar.activation(out=right9[:, g, c, :], in_=z[:], func=SIGMOID, bias=column(2 * c + g))
-            low_of[n] = (turn7, right8, right9)
-
-        def reach7_transpose(n):
-            reach7 = reach7_of[n]
-            banks = []
-            for g in range(2):
-                pt = psum_pt.tile([P, CHUNK], F32)
-                for q in range(ROW_TILES):
-                    nc.tensor.transpose(
-                        out=pt[:, P * q : P * q + P],
-                        in_=reach7[:, q, P * g : P * g + P],
-                        identity=ident[:],
-                    )
-                banks.append(pt)
-            pt_of[n] = banks
-
-        minus9_of = {}
-
-        def reach_8_9(n):
-            turn7, right8, right9 = low_of[n]
-            minus8 = work.tile([P, 2, CHUNK], F32)
-            for g in range(2):
-                nc.vector.scalar_tensor_tensor(
-                    out=minus8[:, g, :], in0=pt_of[n][g][:], scalar=-1.0, in1=turn7[:, g, :], op0=ALU.mult, op1=ALU.mult
-                )
-            minus9 = work.tile([P, 2, 2, CHUNK], F32)
-            nc.vector.tensor_tensor(out=minus9[:, :, 1, :], in0=minus8[:], in1=right8[:], op=ALU.mult)
-            nc.vector.tensor_tensor(out=minus9[:, :, 0, :], in0=minus8[:], in1=minus9[:, :, 1, :], op=ALU.subtract)
-            minus9_of[n] = minus9
-
+        reach9_of = {}
+        probs_of = {}
         pq_of = {}
 
-        def leaf_probs(n):
-            right9 = low_of[n][2]
-            minus9 = minus9_of[n]
-            probs = work.tile([P, PASSES, CHUNK, 4], BF16, align_bytes=64)
+        def low_open(n):
+            turn7 = work.tile([P, 2, CHUNK], F32)
+            right8 = work.tile([P, 2, CHUNK], F32)
+            turn9 = work.tile([P, 2, 4, CHUNK], F32)
+            low_of[n] = (turn7, right8, turn9)
+
+        def low_turn(n, slot, woven, q, k):
+            if live(n):
+                xc, xs = xq_of[n]
+                turn7, right8, turn9 = low_of[n]
+                z = psum_stream.tile([P, CHUNK], F32, name="stream")
+            for g in range(PASSES):
+                if live(n):
+                    nc.tensor.matmul_mx(
+                        out=z[:],
+                        lhsT=wc[:, g, P * slot : P * slot + P].bitcast(FP8X4),
+                        lhsT_scale=ws[:, g, P * slot : P * slot + P],
+                        rhs=xc[:, g, :].bitcast(FP8X4),
+                        rhs_scale=xs[:, g, :],
+                        start=(g == 0),
+                        stop=(g == PASSES - 1),
+                    )
+                top_pass(woven, q, k + g)
+            if not live(n):
+                return
+            if slot < 2:
+                nc.scalar.activation(
+                    out=turn7[:, slot, :], in_=z[:], func=SIGMOID, bias=column(64 + slot), scale=column(96)
+                )
+            elif slot < 4:
+                nc.scalar.activation(out=right8[:, slot - 2, :], in_=z[:], func=SIGMOID, bias=column(32 + slot - 2))
+            else:
+                c, g9 = divmod(slot - 4, 2)
+                nc.scalar.activation(out=turn9[:, g9, 2 * c + 1, :], in_=z[:], func=SIGMOID, bias=column(slot - 4))
+
+        def reach7_transpose(n):
+            pt = psum_pt.tile([P, 2, CHUNK], F32)
+            for g in range(2):
+                for q in range(ROW_TILES):
+                    nc.tensor.transpose(
+                        out=pt[:, g, P * q : P * q + P],
+                        in_=reach7_of[n][:, q, P * g : P * g + P],
+                        identity=ident[:],
+                    )
+            pt_of[n] = pt
+
+        def reach_8_9(n):
+            turn7, right8, turn9 = low_of[n]
+            reach8 = work.tile([P, 2, CHUNK], F32)
+            nc.vector.tensor_tensor(out=reach8[:], in0=pt_of[n][:], in1=turn7[:], op=ALU.mult)
+            reach9 = work.tile([P, 2, 2, CHUNK], F32)
+            nc.vector.tensor_tensor(out=reach9[:, :, 1, :], in0=reach8[:], in1=right8[:], op=ALU.mult)
+            nc.vector.tensor_tensor(out=reach9[:, :, 0, :], in0=reach8[:], in1=reach9[:, :, 1, :], op=ALU.subtract)
+            reach9_of[n] = reach9
+            both = turn9[:].rearrange("p g (c e) b -> p (g c) e b", e=2)
+            nc.vector.tensor_scalar(
+                out=both[:, :, 0, :], in0=both[:, :, 1, :], scalar1=-1.0, scalar2=1.0, op0=ALU.mult, op1=ALU.add
+            )
+            probs_of[n] = work.tile([P, PASSES, CHUNK, 4], BF16, align_bytes=64, name="probs")
             pc = work.tile([P, PASSES, CHUNK], U32, align_bytes=64)
             ps = work.tile([P, PASSES, CHUNK], U8, align_bytes=64)
-            for h in range(2):
-                cols = slice(HALF * h, HALF * h + HALF)
-                for g in range(PASSES):
-                    pairs = probs[:, g, cols, :].rearrange("p b (c e) -> p b c e", e=2)
-                    turn_right = right9[:, g, :, cols].rearrange("p c b -> p b c")
-                    parent = minus9[:, g, :, cols].rearrange("p c b -> p b c")
-                    nc.vector.scalar_tensor_tensor(
-                        out=pairs[:, :, :, 1], in0=turn_right, scalar=-1.0, in1=parent, op0=ALU.mult, op1=ALU.mult
-                    )
-                    nc.vector.scalar_tensor_tensor(
-                        out=pairs[:, :, :, 0], in0=turn_right, scalar=1.0, in1=parent, op0=ALU.subtract, op1=ALU.mult
-                    )
-                for g in range(PASSES):
-                    nc.vector.quantize_mx(
-                        out=pc[:, g, cols].bitcast(FP8X4),
-                        scales=ps[:, g, cols],
-                        in_=probs[:, g, cols, :].rearrange("p b t -> p (b t)"),
-                    )
             pq_of[n] = (pc, ps)
 
-        def leaves(n):
+        def leaf_probs(n, h):
+            turn9 = low_of[n][2]
             pc, ps = pq_of[n]
-            for q in range(ROW_TILES):
+            cols = slice(HALF * h, HALF * h + HALF)
+            for g in range(PASSES):
+                nc.vector.tensor_tensor(
+                    out=probs_of[n][:, g, cols, :].rearrange("p b (c e) -> p b c e", e=2),
+                    in0=reach9_of[n][:, g, :, cols].rearrange("p c b -> p b c").unsqueeze(3).to_broadcast([P, HALF, 2, 2]),
+                    in1=turn9[:, g, :, cols].rearrange("p (c e) b -> p b c e", e=2),
+                    op=ALU.mult,
+                )
+            for g in range(PASSES):
+                nc.vector.quantize_mx(
+                    out=pc[:, g, cols].bitcast(FP8X4),
+                    scales=ps[:, g, cols],
+                    in_=probs_of[n][:, g, cols, :].rearrange("p b t -> p (b t)"),
+                )
+
+        def leaves(n, q, woven):
+            if live(n):
+                pc, ps = pq_of[n]
                 rows = ostage.tile([P, CLASSES], F32)
-                for half in range(2):
+            for half in range(2):
+                if live(n):
                     acc = psum_o.tile([P, 512], F32)
-                    for g in range(PASSES):
+                for g in range(PASSES):
+                    if live(n):
                         nc.tensor.matmul_mx(
                             out=acc[:],
                             lhsT=pc[:, g, P * q : P * q + P].bitcast(FP8X4),
@@ -320,39 +326,46 @@ def tile_treemodel_kernel(tc, x, W_gate, b_gate, leaf_logits_words, leaf_logits_
                             start=(g == 0),
                             stop=(g == PASSES - 1),
                         )
+                    top_pass(woven, q, PASSES * half + g)
+                if live(n):
                     nc.scalar.copy(out=rows[:, 512 * half : 512 * half + 512], in_=acc[:])
+            if live(n):
                 nc.sync.dma_start(out=out_tiles[n, q], in_=rows[:])
 
-        def live(n):
-            return 0 <= n < CHUNKS
-
+        x_transpose(0)
         for n in range(-2, CHUNKS + 1):
             if live(n):
                 reach_8_9(n)
-            if live(n - 1):
-                leaves(n - 1)
-            if live(n + 1):
-                top_sweep(n + 1)
+                leaf_probs(n, 0)
             if live(n + 2):
-                x_transpose(n + 2)
+                top_open(n + 2)
             if n == -2:
                 spread_bias()
                 regroup_levels_7_8(0)
-            if n == -1:
-                for g in range(PASSES):
-                    regroup_level_9(g)
-                for g in range(PASSES):
-                    quantise_w(g, 512)
-            if live(n):
-                leaf_probs(n)
-            if live(n + 1):
-                low_turns(n + 1)
-                reach7_transpose(n + 1)
-            if live(n + 2):
-                x_quantise(n + 2)
-            if n == -2:
+                x_quantise(0)
                 regroup_levels_7_8(1)
                 for g in range(PASSES):
                     quantise_w(g, 0)
+                for g in range(PASSES):
+                    regroup_level_9(g)
+            if live(n + 1):
+                top_sweep(n + 1)
+            if live(n + 1):
+                low_open(n + 1)
+            if live(n):
+                leaf_probs(n, 1)
+            for q in range(ROW_TILES):
+                if q == ROW_TILES - 1 and live(n + 3):
+                    x_transpose(n + 3)
+                leaves(n - 1, q, n + 2)
+                for s in range(SLOTS_PER_ROUND):
+                    low_turn(n + 1, SLOTS_PER_ROUND * q + s, n + 2, q, 2 * PASSES + PASSES * s)
+                if q == 1 and live(n + 1):
+                    reach7_transpose(n + 1)
             if live(n + 2):
-                top_logits(n + 2)
+                top_turns(n + 2)
+            if n == -2:
+                for g in range(PASSES):
+                    quantise_w(g, 512)
+            if live(n + 2) and n > -2:
+                x_quantise(n + 2)

@@ -17,14 +17,12 @@ BATCH = 2048
 FEATURES = 1024
 CLASSES = 1024
 PASSES = 2
-CHUNK = 256
+CHUNK = 512
 HALF = CHUNK // 2
 ROW_TILES = CHUNK // P
 CHUNKS = BATCH // CHUNK
 TOP = 128
 SLOTS = 8
-SLOTS_PER_ROUND = SLOTS // ROW_TILES
-PLAIN_PASSES = 9
 
 FLOPS = 2 * BATCH * FEATURES * (TOP + 896) + 2 * BATCH * 1024 * CLASSES
 
@@ -36,10 +34,9 @@ def tile_treemodel_kernel(tc, x, W_gate, b_gate, leaf_logits_words, leaf_logits_
         xin = ctx.enter_context(tc.tile_pool(name="xin", bufs=CHUNKS))
         work = ctx.enter_context(tc.tile_pool(name="work", bufs=2))
         ostage = ctx.enter_context(tc.tile_pool(name="ostage", bufs=4))
-        psum_stream = ctx.enter_context(tc.psum_pool(name="psum_stream", bufs=3))
-        psum_top = ctx.enter_context(tc.psum_pool(name="psum_top", bufs=2))
-        psum_pt = ctx.enter_context(tc.psum_pool(name="psum_pt", bufs=1))
-        psum_o = ctx.enter_context(tc.psum_pool(name="psum_o", bufs=2))
+        psum_stream = ctx.enter_context(tc.psum_pool(name="psum_stream", bufs=5))
+        psum_top = ctx.enter_context(tc.psum_pool(name="psum_top", bufs=1))
+        psum_pt = ctx.enter_context(tc.psum_pool(name="psum_pt", bufs=2))
         ctx.enter_context(tc.manual_schedule())
 
         x_chunks = x.rearrange("(n p q) k -> n p q k", p=P, q=ROW_TILES)
@@ -64,11 +61,18 @@ def tile_treemodel_kernel(tc, x, W_gate, b_gate, leaf_logits_words, leaf_logits_
             x_rows.append(xin.tile([P, ROW_TILES, FEATURES], BF16, name="x_sb"))
         w_raw = const.tile([P, 4, 2, 1024], BF16)
         w_rows = W_gate.rearrange("(a p e) c -> a p e c", a=4, p=P, e=2)
-        nc.sync.dma_start(out=x_rows[0][:], in_=x_chunks[0])
+        w_top = const.tile([P, 4, 2, TOP], BF16)
+        top_rows = W_gate.rearrange("(a p e) c -> e p a c", a=4, p=P, e=2)
+        nc.sync.dma_start(out=x_rows[0][:, 0:2, :], in_=x_chunks[0][:, 0:2, :])
+        for e in range(2):
+            nc.sync.dma_start(out=w_top[:, :, e, :], in_=top_rows[e][:, :, 0:TOP])
+        nc.sync.dma_start(out=x_rows[0][:, 2:4, :], in_=x_chunks[0][:, 2:4, :])
+        nc.sync.dma_start(out=x_rows[1][:], in_=x_chunks[1])
         for a in range(4):
             nc.sync.dma_start(out=w_raw[:, a, :, 0:1023], in_=w_rows[a])
         w_planes = w_raw[:].rearrange("p (g u) e c -> p g (u e) c", g=PASSES)
-        for n in range(1, CHUNKS):
+        top_planes = w_top[:].rearrange("p (g u) e c -> p g (u e) c", g=PASSES)
+        for n in range(2, CHUNKS):
             nc.sync.dma_start(out=x_rows[n][:], in_=x_chunks[n])
 
         leaf_scales = const.tile([P, PASSES, CLASSES], U8, align_bytes=64)
@@ -140,118 +144,125 @@ def tile_treemodel_kernel(tc, x, W_gate, b_gate, leaf_logits_words, leaf_logits_
         xg_of = {}
         xq_of = {}
 
-        def x_transpose(n):
-            x_sb = x_rows[n]
-            xg = work.tile([P, PASSES, CHUNK, 4], BF16, align_bytes=64, bufs=3)
-            for g in range(PASSES):
-                xt = psum_stream.tile([P, 2, CHUNK], F32, name="stream")
-                for u in range(2):
-                    for q in range(ROW_TILES):
-                        first = 256 * g + 128 * u
-                        nc.tensor.transpose(
-                            out=xt[:, u, P * q : P * q + P],
-                            in_=x_sb[:, q, :].bitcast(F32)[:, first : first + P],
-                            identity=ident[:],
-                        )
-                nc.scalar.copy(
-                    out=xg[:, g].rearrange("p b t -> p (b t)").bitcast(F32).rearrange("p (b u) -> p b u", u=2),
-                    in_=xt[:].rearrange("p u b -> p b u"),
-                )
-            xg_of[n] = xg
+        def x_transpose(n, h, g):
+            if not live(n):
+                return
+            if h == 0 and g == 0:
+                xg_of[n] = work.tile([P, PASSES, CHUNK, 4], BF16, align_bytes=64, name="xg")
+            xt = psum_stream.tile([P, 2, HALF], F32, name="stream")
+            for u in range(2):
+                for qq in range(2):
+                    first = 256 * g + 128 * u
+                    nc.tensor.transpose(
+                        out=xt[:, u, P * qq : P * qq + P],
+                        in_=x_rows[n][:, 2 * h + qq, :].bitcast(F32)[:, first : first + P],
+                        identity=ident[:],
+                    )
+            dst = xg_of[n][:, g, HALF * h : HALF * h + HALF, :].rearrange("p b t -> p (b t)").bitcast(F32)
+            nc.scalar.copy(out=dst.rearrange("p (b u) -> p b u", u=2), in_=xt[:].rearrange("p u b -> p b u"))
 
-        def x_quantise(n):
-            xc = work.tile([P, PASSES, CHUNK], U32, align_bytes=64)
-            xs = work.tile([P, PASSES, CHUNK], U8, align_bytes=64)
-            for g in range(PASSES):
-                nc.vector.quantize_mx(
-                    out=xc[:, g, :].bitcast(FP8X4),
-                    scales=xs[:, g, :],
-                    in_=xg_of[n][:, g].rearrange("p b t -> p (b t)"),
-                )
-            xq_of[n] = (xc, xs)
+        def x_quantise(n, g):
+            if not live(n):
+                return
+            if g == 0:
+                xc = work.tile([P, PASSES, CHUNK], U32, align_bytes=64)
+                xs = work.tile([P, PASSES, CHUNK], U8, align_bytes=64)
+                xq_of[n] = (xc, xs)
+            xc, xs = xq_of[n]
+            nc.vector.quantize_mx(
+                out=xc[:, g, :].bitcast(FP8X4),
+                scales=xs[:, g, :],
+                in_=xg_of[n][:, g].rearrange("p b t -> p (b t)"),
+            )
 
-        top_of = {}
         turn_of = {}
         reach7_of = {}
 
-        def top_open(n):
-            top_of[n] = psum_top.tile([P, ROW_TILES, TOP], F32, name="top")
+        top_of = {}
 
-        def top_pass(n, q, k):
-            if not live(n) or k >= PLAIN_PASSES:
+        def top_logits(n, q):
+            if not live(n):
                 return
-            if k < PLAIN_PASSES - 1:
-                g, t = divmod(k, 4)
-                nc.tensor.matmul(
-                    out=top_of[n][:, q, :],
-                    lhsT=xg_of[n][:, g, P * q : P * q + P, t],
-                    rhs=w_planes[:, g, t, 0:TOP],
-                    start=(k == 0),
-                    stop=False,
-                )
-            else:
-                nc.tensor.matmul(out=top_of[n][:, q, :], lhsT=ones[:], rhs=bias_row[:], start=False, stop=True)
+            if q == 0:
+                top_of[n] = psum_top.tile([P, ROW_TILES, TOP], F32, name="top")
+            for g in range(PASSES):
+                for t in range(4):
+                    nc.tensor.matmul(
+                        out=top_of[n][:, q, :],
+                        lhsT=xg_of[n][:, g, P * q : P * q + P, t],
+                        rhs=top_planes[:, g, t, :],
+                        start=(g == 0 and t == 0),
+                        stop=False,
+                    )
+            nc.tensor.matmul(out=top_of[n][:, q, :], lhsT=ones[:], rhs=bias_row[:], start=False, stop=True)
 
         def top_turns(n):
+            if not live(n):
+                return
             turn = work.tile([P, 2, ROW_TILES, TOP], F32)
             nc.scalar.activation(out=turn[:, 1], in_=top_of[n][:], func=SIGMOID)
             nc.scalar.activation(out=turn[:, 0], in_=top_of[n][:], func=SIGMOID, scale=-1.0)
             turn_of[n] = turn
 
-        def top_sweep(n):
+        reach_of = {}
+
+        def sweep_level(n, level):
+            if not live(n):
+                return
             turn = turn_of[n]
-            reach = turn[:, :, :, 0].rearrange("p j q -> p q j")
-            for level in range(1, 6):
-                nodes = 2**level
-                children = work.tile([P, ROW_TILES, 2 * nodes], F32, name="reach%d" % (level + 1))
-                nc.vector.tensor_tensor(
-                    out=children[:].rearrange("p q (j c) -> p q j c", c=2),
-                    in0=reach.unsqueeze(3).to_broadcast([P, ROW_TILES, nodes, 2]),
-                    in1=turn[:, :, :, nodes - 1 : 2 * nodes - 1].rearrange("p c q j -> p q j c"),
-                    op=ALU.mult,
-                )
-                reach = children[:]
-            reach7 = work.tile([P, ROW_TILES, 256], F32)
-            for q in range(ROW_TILES):
-                nc.vector.tensor_tensor(
-                    out=reach7[:, q, :].rearrange("p (j c d) -> p j c d", c=2, d=2),
-                    in0=reach[:, q, :].unsqueeze(2).unsqueeze(3).to_broadcast([P, 64, 2, 2]),
-                    in1=turn[:, :, q, 63:127].rearrange("p c j -> p j c").unsqueeze(3).to_broadcast([P, 64, 2, 2]),
-                    op=ALU.mult,
-                )
-            reach7_of[n] = reach7
+            nodes = 2**level
+            if level == 1:
+                reach = turn[:, :, :, 0].rearrange("p j q -> p q j")
+            else:
+                reach = reach_of[n][:]
+            children = work.tile([P, ROW_TILES, 2 * nodes], F32, name="reach%d" % (level + 1))
+            nc.vector.tensor_tensor(
+                out=children[:].rearrange("p q (j c) -> p q j c", c=2),
+                in0=reach.unsqueeze(3).to_broadcast([P, ROW_TILES, nodes, 2]),
+                in1=turn[:, :, :, nodes - 1 : 2 * nodes - 1].rearrange("p c q j -> p q j c"),
+                op=ALU.mult,
+            )
+            reach_of[n] = children
+
+        def sweep_last(n, q):
+            if not live(n):
+                return
+            if q == 0:
+                reach7_of[n] = work.tile([P, ROW_TILES, 256], F32, name="reach7")
+            nc.vector.tensor_tensor(
+                out=reach7_of[n][:, q, :].rearrange("p (j c d) -> p j c d", c=2, d=2),
+                in0=reach_of[n][:, q, :].unsqueeze(2).unsqueeze(3).to_broadcast([P, 64, 2, 2]),
+                in1=turn_of[n][:, :, q, 63:127].rearrange("p c j -> p j c").unsqueeze(3).to_broadcast([P, 64, 2, 2]),
+                op=ALU.mult,
+            )
 
         low_of = {}
         pt_of = {}
-        reach9_of = {}
-        probs_of = {}
-        pq_of = {}
 
-        def low_open(n):
-            turn7 = work.tile([P, 2, CHUNK], F32)
-            right8 = work.tile([P, 2, CHUNK], F32)
-            turn9 = work.tile([P, 2, 4, CHUNK], F32)
-            low_of[n] = (turn7, right8, turn9)
-
-        def low_turn(n, slot, woven, q, k):
-            if live(n):
-                xc, xs = xq_of[n]
-                turn7, right8, turn9 = low_of[n]
-                z = psum_stream.tile([P, CHUNK], F32, name="stream")
+        def low_logits(xc, xs, slot):
+            z = psum_stream.tile([P, CHUNK], F32, name="stream")
             for g in range(PASSES):
-                if live(n):
-                    nc.tensor.matmul_mx(
-                        out=z[:],
-                        lhsT=wc[:, g, P * slot : P * slot + P].bitcast(FP8X4),
-                        lhsT_scale=ws[:, g, P * slot : P * slot + P],
-                        rhs=xc[:, g, :].bitcast(FP8X4),
-                        rhs_scale=xs[:, g, :],
-                        start=(g == 0),
-                        stop=(g == PASSES - 1),
-                    )
-                top_pass(woven, q, k + g)
+                nc.tensor.matmul_mx(
+                    out=z[:],
+                    lhsT=wc[:, g, P * slot : P * slot + P].bitcast(FP8X4),
+                    lhsT_scale=ws[:, g, P * slot : P * slot + P],
+                    rhs=xc[:, g, :].bitcast(FP8X4),
+                    rhs_scale=xs[:, g, :],
+                    start=(g == 0),
+                    stop=(g == PASSES - 1),
+                )
+            return z
+
+        def low_turn(n, slot):
             if not live(n):
                 return
+            if slot == 0:
+                turn7 = work.tile([P, 2, CHUNK], F32)
+                right8 = work.tile([P, 2, CHUNK], F32)
+                right9 = work.tile([P, 2, 2, CHUNK], F32)
+                low_of[n] = (turn7, right8, right9)
+            turn7, right8, right9 = low_of[n]
+            z = low_logits(xq_of[n][0], xq_of[n][1], slot)
             if slot < 2:
                 nc.scalar.activation(
                     out=turn7[:, slot, :], in_=z[:], func=SIGMOID, bias=column(64 + slot), scale=column(96)
@@ -260,112 +271,146 @@ def tile_treemodel_kernel(tc, x, W_gate, b_gate, leaf_logits_words, leaf_logits_
                 nc.scalar.activation(out=right8[:, slot - 2, :], in_=z[:], func=SIGMOID, bias=column(32 + slot - 2))
             else:
                 c, g9 = divmod(slot - 4, 2)
-                nc.scalar.activation(out=turn9[:, g9, 2 * c + 1, :], in_=z[:], func=SIGMOID, bias=column(slot - 4))
+                nc.scalar.activation(out=right9[:, g9, c, :], in_=z[:], func=SIGMOID, bias=column(slot - 4))
 
         def reach7_transpose(n):
-            pt = psum_pt.tile([P, 2, CHUNK], F32)
+            reach7 = reach7_of[n]
+            banks = []
             for g in range(2):
+                pt = psum_pt.tile([P, CHUNK], F32)
                 for q in range(ROW_TILES):
                     nc.tensor.transpose(
-                        out=pt[:, g, P * q : P * q + P],
-                        in_=reach7_of[n][:, q, P * g : P * g + P],
+                        out=pt[:, P * q : P * q + P],
+                        in_=reach7[:, q, P * g : P * g + P],
                         identity=ident[:],
                     )
-            pt_of[n] = pt
+                banks.append(pt)
+            pt_of[n] = banks
 
-        def reach_8_9(n):
-            turn7, right8, turn9 = low_of[n]
-            reach8 = work.tile([P, 2, CHUNK], F32)
-            nc.vector.tensor_tensor(out=reach8[:], in0=pt_of[n][:], in1=turn7[:], op=ALU.mult)
-            reach9 = work.tile([P, 2, 2, CHUNK], F32)
-            nc.vector.tensor_tensor(out=reach9[:, :, 1, :], in0=reach8[:], in1=right8[:], op=ALU.mult)
-            nc.vector.tensor_tensor(out=reach9[:, :, 0, :], in0=reach8[:], in1=reach9[:, :, 1, :], op=ALU.subtract)
-            reach9_of[n] = reach9
-            both = turn9[:].rearrange("p g (c e) b -> p (g c) e b", e=2)
-            nc.vector.tensor_scalar(
-                out=both[:, :, 0, :], in0=both[:, :, 1, :], scalar1=-1.0, scalar2=1.0, op0=ALU.mult, op1=ALU.add
+        minus8_of = {}
+        minus9_of = {}
+        probs_of = {}
+        pq_of = {}
+
+        def reach8(n, g):
+            if g == 0:
+                minus8_of[n] = work.tile([P, 2, CHUNK], F32, name="minus8")
+            nc.vector.scalar_tensor_tensor(
+                out=minus8_of[n][:, g, :], in0=pt_of[n][g][:], scalar=-1.0, in1=low_of[n][0][:, g, :],
+                op0=ALU.mult, op1=ALU.mult,
+            )
+
+        def reach9_right(n):
+            minus9_of[n] = work.tile([P, 2, 2, CHUNK], F32, name="minus9")
+            nc.vector.tensor_tensor(out=minus9_of[n][:, :, 1, :], in0=minus8_of[n][:], in1=low_of[n][1][:], op=ALU.mult)
+
+        def reach9_left(n):
+            nc.vector.tensor_tensor(
+                out=minus9_of[n][:, :, 0, :], in0=minus8_of[n][:], in1=minus9_of[n][:, :, 1, :], op=ALU.subtract
             )
             probs_of[n] = work.tile([P, PASSES, CHUNK, 4], BF16, align_bytes=64, name="probs")
             pc = work.tile([P, PASSES, CHUNK], U32, align_bytes=64)
             ps = work.tile([P, PASSES, CHUNK], U8, align_bytes=64)
             pq_of[n] = (pc, ps)
 
-        def leaf_probs(n, h):
-            turn9 = low_of[n][2]
-            pc, ps = pq_of[n]
+        def leaf_probs(n, h, g, e):
             cols = slice(HALF * h, HALF * h + HALF)
-            for g in range(PASSES):
-                nc.vector.tensor_tensor(
-                    out=probs_of[n][:, g, cols, :].rearrange("p b (c e) -> p b c e", e=2),
-                    in0=reach9_of[n][:, g, :, cols].rearrange("p c b -> p b c").unsqueeze(3).to_broadcast([P, HALF, 2, 2]),
-                    in1=turn9[:, g, :, cols].rearrange("p (c e) b -> p b c e", e=2),
-                    op=ALU.mult,
+            pairs = probs_of[n][:, g, cols, :].rearrange("p b (c e) -> p b c e", e=2)
+            turn_right = low_of[n][2][:, g, :, cols].rearrange("p c b -> p b c")
+            parent = minus9_of[n][:, g, :, cols].rearrange("p c b -> p b c")
+            if e == 1:
+                nc.vector.scalar_tensor_tensor(
+                    out=pairs[:, :, :, 1], in0=turn_right, scalar=-1.0, in1=parent, op0=ALU.mult, op1=ALU.mult
                 )
-            for g in range(PASSES):
-                nc.vector.quantize_mx(
-                    out=pc[:, g, cols].bitcast(FP8X4),
-                    scales=ps[:, g, cols],
-                    in_=probs_of[n][:, g, cols, :].rearrange("p b t -> p (b t)"),
+            else:
+                nc.vector.scalar_tensor_tensor(
+                    out=pairs[:, :, :, 0], in0=turn_right, scalar=1.0, in1=parent, op0=ALU.subtract, op1=ALU.mult
                 )
 
-        def leaves(n, q, woven):
-            if live(n):
-                pc, ps = pq_of[n]
-                rows = ostage.tile([P, CLASSES], F32)
-            for half in range(2):
-                if live(n):
-                    acc = psum_o.tile([P, 512], F32)
-                for g in range(PASSES):
-                    if live(n):
-                        nc.tensor.matmul_mx(
-                            out=acc[:],
-                            lhsT=pc[:, g, P * q : P * q + P].bitcast(FP8X4),
-                            lhsT_scale=ps[:, g, P * q : P * q + P],
-                            rhs=leaf_words[:, g, 2048 * half : 2048 * half + 2048].bitcast(FP8X4),
-                            rhs_scale=leaf_scales[:, g, 512 * half : 512 * half + 512],
-                            start=(g == 0),
-                            stop=(g == PASSES - 1),
-                        )
-                    top_pass(woven, q, PASSES * half + g)
-                if live(n):
-                    nc.scalar.copy(out=rows[:, 512 * half : 512 * half + 512], in_=acc[:])
-            if live(n):
-                nc.sync.dma_start(out=out_tiles[n, q], in_=rows[:])
+        def leaf_quantise(n, h, g):
+            cols = slice(HALF * h, HALF * h + HALF)
+            pc, ps = pq_of[n]
+            nc.vector.quantize_mx(
+                out=pc[:, g, cols].bitcast(FP8X4),
+                scales=ps[:, g, cols],
+                in_=probs_of[n][:, g, cols, :].rearrange("p b t -> p (b t)"),
+            )
 
-        x_transpose(0)
-        for n in range(-2, CHUNKS + 1):
+        rows_of = {}
+
+        def leaves(n, q, half):
+            if not live(n):
+                return
+            pc, ps = pq_of[n]
+            if half == 0:
+                rows_of[n] = ostage.tile([P, CLASSES], F32, name="rows")
+            acc = psum_stream.tile([P, 512], F32, name="stream")
+            for g in range(PASSES):
+                nc.tensor.matmul_mx(
+                    out=acc[:],
+                    lhsT=pc[:, g, P * q : P * q + P].bitcast(FP8X4),
+                    lhsT_scale=ps[:, g, P * q : P * q + P],
+                    rhs=leaf_words[:, g, 2048 * half : 2048 * half + 2048].bitcast(FP8X4),
+                    rhs_scale=leaf_scales[:, g, 512 * half : 512 * half + 512],
+                    start=(g == 0),
+                    stop=(g == PASSES - 1),
+                )
+            nc.scalar.copy(out=rows_of[n][:, 512 * half : 512 * half + 512], in_=acc[:])
+            if half == 1:
+                nc.sync.dma_start(out=out_tiles[n, q], in_=rows_of[n][:])
+
+        def vector_period(n):
             if live(n):
-                reach_8_9(n)
-                leaf_probs(n, 0)
-            if live(n + 2):
-                top_open(n + 2)
-            if n == -2:
-                spread_bias()
-                regroup_levels_7_8(0)
-                x_quantise(0)
-                regroup_levels_7_8(1)
-                for g in range(PASSES):
-                    quantise_w(g, 0)
-                for g in range(PASSES):
-                    regroup_level_9(g)
-            if live(n + 1):
-                top_sweep(n + 1)
-            if live(n + 1):
-                low_open(n + 1)
+                reach8(n, 0)
+            sweep_level(n + 1, 1)
             if live(n):
-                leaf_probs(n, 1)
+                reach8(n, 1)
+            sweep_level(n + 1, 2)
+            if live(n):
+                reach9_right(n)
+            sweep_level(n + 1, 3)
+            if live(n):
+                reach9_left(n)
+            sweep_level(n + 1, 4)
+            x_quantise(n + 2, 0)
+            sweep_level(n + 1, 5)
+            x_quantise(n + 2, 1)
+            for h in range(2):
+                for g in range(PASSES):
+                    for e in range(2):
+                        if h == 0:
+                            sweep_last(n + 1, 2 * g + e)
+                        if live(n):
+                            leaf_probs(n, h, g, e)
+                if live(n):
+                    for g in range(PASSES):
+                        leaf_quantise(n, h, g)
+
+        def front(n_x, n_top):
             for q in range(ROW_TILES):
-                if q == ROW_TILES - 1 and live(n + 3):
-                    x_transpose(n + 3)
-                leaves(n - 1, q, n + 2)
-                for s in range(SLOTS_PER_ROUND):
-                    low_turn(n + 1, SLOTS_PER_ROUND * q + s, n + 2, q, 2 * PASSES + PASSES * s)
-                if q == 1 and live(n + 1):
-                    reach7_transpose(n + 1)
-            if live(n + 2):
-                top_turns(n + 2)
-            if n == -2:
+                x_transpose(n_x, q // 2, q % 2)
+                top_logits(n_top, q)
+            top_turns(n_top)
+
+        front(0, -1)
+        spread_bias()
+        front(1, 0)
+        x_quantise(0, 0)
+        x_quantise(0, 1)
+        for g in range(PASSES):
+            regroup_levels_7_8(g)
+        for g in range(PASSES):
+            quantise_w(g, 0)
+        for g in range(PASSES):
+            regroup_level_9(g)
+        for n in range(-1, CHUNKS + 1):
+            vector_period(n)
+            if n == -1:
                 for g in range(PASSES):
                     quantise_w(g, 512)
-            if live(n + 2) and n > -2:
-                x_quantise(n + 2)
+            front(n + 3, n + 2)
+            for i in range(SLOTS):
+                leaves(n - 1, i // 2, i % 2)
+                low_turn(n + 1, i)
+                if i == 3 and live(n + 1):
+                    reach7_transpose(n + 1)

@@ -31,7 +31,7 @@ def tile_treemodel_kernel(tc, x, W_gate, b_gate, leaf_logits_words, leaf_logits_
     nc = tc.nc
     with ExitStack() as ctx:
         const = ctx.enter_context(tc.tile_pool(name="const", bufs=1))
-        xin = ctx.enter_context(tc.tile_pool(name="xin", bufs=CHUNKS))
+        xin = ctx.enter_context(tc.tile_pool(name="xin", bufs=3))
         work = ctx.enter_context(tc.tile_pool(name="work", bufs=2))
         ostage = ctx.enter_context(tc.tile_pool(name="ostage", bufs=4))
         psum_stream = ctx.enter_context(tc.psum_pool(name="psum_stream", bufs=5))
@@ -56,24 +56,29 @@ def tile_treemodel_kernel(tc, x, W_gate, b_gate, leaf_logits_words, leaf_logits_
         nc.scalar.dma_start(out=b_src[32:34, 0:128], in_=b_gate[255:511].rearrange("(g m) -> g m", g=2))
         nc.scalar.dma_start(out=b_src[64:66, 0:64], in_=b_gate[127:255].rearrange("(g j) -> g j", g=2))
 
-        x_rows = []
-        for n in range(CHUNKS):
-            x_rows.append(xin.tile([P, ROW_TILES, FEATURES], BF16, name="x_sb"))
+        x_rows = {}
+
+        def x_load(n, pieces):
+            x_rows[n] = xin.tile([P, ROW_TILES, FEATURES], BF16, name="x_sb")
+            step = ROW_TILES // pieces
+            for i in range(pieces):
+                nc.sync.dma_start(
+                    out=x_rows[n][:, step * i : step * i + step, :], in_=x_chunks[n][:, step * i : step * i + step, :]
+                )
+
         w_raw = const.tile([P, 4, 2, 1024], BF16)
         w_rows = W_gate.rearrange("(a p e) c -> a p e c", a=4, p=P, e=2)
         w_top = const.tile([P, 4, 2, TOP], BF16)
         top_rows = W_gate.rearrange("(a p e) c -> e p a c", a=4, p=P, e=2)
-        nc.sync.dma_start(out=x_rows[0][:, 0:2, :], in_=x_chunks[0][:, 0:2, :])
+        x_load(0, 2)
         for e in range(2):
             nc.sync.dma_start(out=w_top[:, :, e, :], in_=top_rows[e][:, :, 0:TOP])
-        nc.sync.dma_start(out=x_rows[0][:, 2:4, :], in_=x_chunks[0][:, 2:4, :])
-        nc.sync.dma_start(out=x_rows[1][:], in_=x_chunks[1])
+        x_load(1, 1)
         for a in range(4):
             nc.sync.dma_start(out=w_raw[:, a, :, 0:1023], in_=w_rows[a])
         w_planes = w_raw[:].rearrange("p (g u) e c -> p g (u e) c", g=PASSES)
         top_planes = w_top[:].rearrange("p (g u) e c -> p g (u e) c", g=PASSES)
-        for n in range(2, CHUNKS):
-            nc.sync.dma_start(out=x_rows[n][:], in_=x_chunks[n])
+        x_load(2, 1)
 
         leaf_scales = const.tile([P, PASSES, CLASSES], U8, align_bytes=64)
         nc.vector.memset(leaf_scales[:].rearrange("p g n -> p (g n)").bitcast(I32), 0)
@@ -259,9 +264,9 @@ def tile_treemodel_kernel(tc, x, W_gate, b_gate, leaf_logits_words, leaf_logits_
             if slot == 0:
                 turn7 = work.tile([P, 2, CHUNK], F32)
                 right8 = work.tile([P, 2, CHUNK], F32)
-                right9 = work.tile([P, 2, 2, CHUNK], F32)
-                low_of[n] = (turn7, right8, right9)
-            turn7, right8, right9 = low_of[n]
+                turn9 = work.tile([P, 2, 4, CHUNK], F32)
+                low_of[n] = (turn7, right8, turn9)
+            turn7, right8, turn9 = low_of[n]
             z = low_logits(xq_of[n][0], xq_of[n][1], slot)
             if slot < 2:
                 nc.scalar.activation(
@@ -271,7 +276,7 @@ def tile_treemodel_kernel(tc, x, W_gate, b_gate, leaf_logits_words, leaf_logits_
                 nc.scalar.activation(out=right8[:, slot - 2, :], in_=z[:], func=SIGMOID, bias=column(32 + slot - 2))
             else:
                 c, g9 = divmod(slot - 4, 2)
-                nc.scalar.activation(out=right9[:, g9, c, :], in_=z[:], func=SIGMOID, bias=column(slot - 4))
+                nc.scalar.activation(out=turn9[:, g9, 2 * c + 1, :], in_=z[:], func=SIGMOID, bias=column(slot - 4))
 
         def reach7_transpose(n):
             reach7 = reach7_of[n]
@@ -287,45 +292,44 @@ def tile_treemodel_kernel(tc, x, W_gate, b_gate, leaf_logits_words, leaf_logits_
                 banks.append(pt)
             pt_of[n] = banks
 
-        minus8_of = {}
-        minus9_of = {}
+        reach8_of = {}
+        reach9_of = {}
         probs_of = {}
         pq_of = {}
 
         def reach8(n, g):
             if g == 0:
-                minus8_of[n] = work.tile([P, 2, CHUNK], F32, name="minus8")
-            nc.vector.scalar_tensor_tensor(
-                out=minus8_of[n][:, g, :], in0=pt_of[n][g][:], scalar=-1.0, in1=low_of[n][0][:, g, :],
-                op0=ALU.mult, op1=ALU.mult,
-            )
+                reach8_of[n] = work.tile([P, 2, CHUNK], F32, name="reach8", bufs=1)
+            nc.vector.tensor_tensor(out=reach8_of[n][:, g, :], in0=pt_of[n][g][:], in1=low_of[n][0][:, g, :], op=ALU.mult)
 
         def reach9_right(n):
-            minus9_of[n] = work.tile([P, 2, 2, CHUNK], F32, name="minus9")
-            nc.vector.tensor_tensor(out=minus9_of[n][:, :, 1, :], in0=minus8_of[n][:], in1=low_of[n][1][:], op=ALU.mult)
+            reach9_of[n] = work.tile([P, 2, 2, CHUNK], F32, name="reach9", bufs=1)
+            nc.vector.tensor_tensor(out=reach9_of[n][:, :, 1, :], in0=reach8_of[n][:], in1=low_of[n][1][:], op=ALU.mult)
 
         def reach9_left(n):
             nc.vector.tensor_tensor(
-                out=minus9_of[n][:, :, 0, :], in0=minus8_of[n][:], in1=minus9_of[n][:, :, 1, :], op=ALU.subtract
+                out=reach9_of[n][:, :, 0, :], in0=reach8_of[n][:], in1=reach9_of[n][:, :, 1, :], op=ALU.subtract
             )
-            probs_of[n] = work.tile([P, PASSES, CHUNK, 4], BF16, align_bytes=64, name="probs")
-            pc = work.tile([P, PASSES, CHUNK], U32, align_bytes=64)
-            ps = work.tile([P, PASSES, CHUNK], U8, align_bytes=64)
-            pq_of[n] = (pc, ps)
 
-        def leaf_probs(n, h, g, e):
+        def left_turns(n, g):
+            both = low_of[n][2][:, g].rearrange("p (c e) b -> p c e b", e=2)
+            nc.vector.tensor_scalar(
+                out=both[:, :, 0, :], in0=both[:, :, 1, :], scalar1=-1.0, scalar2=1.0, op0=ALU.mult, op1=ALU.add
+            )
+
+        def leaf_probs(n, h, g):
+            if h == 0 and g == 0:
+                probs_of[n] = work.tile([P, PASSES, CHUNK, 4], BF16, align_bytes=64, name="probs")
+                pc = work.tile([P, PASSES, CHUNK], U32, align_bytes=64)
+                ps = work.tile([P, PASSES, CHUNK], U8, align_bytes=64)
+                pq_of[n] = (pc, ps)
             cols = slice(HALF * h, HALF * h + HALF)
-            pairs = probs_of[n][:, g, cols, :].rearrange("p b (c e) -> p b c e", e=2)
-            turn_right = low_of[n][2][:, g, :, cols].rearrange("p c b -> p b c")
-            parent = minus9_of[n][:, g, :, cols].rearrange("p c b -> p b c")
-            if e == 1:
-                nc.vector.scalar_tensor_tensor(
-                    out=pairs[:, :, :, 1], in0=turn_right, scalar=-1.0, in1=parent, op0=ALU.mult, op1=ALU.mult
-                )
-            else:
-                nc.vector.scalar_tensor_tensor(
-                    out=pairs[:, :, :, 0], in0=turn_right, scalar=1.0, in1=parent, op0=ALU.subtract, op1=ALU.mult
-                )
+            nc.vector.tensor_tensor(
+                out=probs_of[n][:, g, cols, :].rearrange("p b (c e) -> p b c e", e=2),
+                in0=reach9_of[n][:, g, :, cols].rearrange("p c b -> p b c").unsqueeze(3).to_broadcast([P, HALF, 2, 2]),
+                in1=low_of[n][2][:, g, :, cols].rearrange("p (c e) b -> p b c e", e=2),
+                op=ALU.mult,
+            )
 
         def leaf_quantise(n, h, g):
             cols = slice(HALF * h, HALF * h + HALF)
@@ -372,16 +376,20 @@ def tile_treemodel_kernel(tc, x, W_gate, b_gate, leaf_logits_words, leaf_logits_
             if live(n):
                 reach9_left(n)
             sweep_level(n + 1, 4)
-            x_quantise(n + 2, 0)
+            if live(n):
+                left_turns(n, 0)
             sweep_level(n + 1, 5)
+            if live(n):
+                left_turns(n, 1)
+            x_quantise(n + 2, 0)
             x_quantise(n + 2, 1)
             for h in range(2):
                 for g in range(PASSES):
-                    for e in range(2):
-                        if h == 0:
-                            sweep_last(n + 1, 2 * g + e)
-                        if live(n):
-                            leaf_probs(n, h, g, e)
+                    if h == 0:
+                        sweep_last(n + 1, 2 * g)
+                        sweep_last(n + 1, 2 * g + 1)
+                    if live(n):
+                        leaf_probs(n, h, g)
                 if live(n):
                     for g in range(PASSES):
                         leaf_quantise(n, h, g)
@@ -394,6 +402,7 @@ def tile_treemodel_kernel(tc, x, W_gate, b_gate, leaf_logits_words, leaf_logits_
 
         front(0, -1)
         spread_bias()
+        x_load(3, 1)
         front(1, 0)
         x_quantise(0, 0)
         x_quantise(0, 1)

@@ -31,7 +31,7 @@ def tile_treemodel_kernel(tc, x, W_gate, b_gate, leaf_logits_words, leaf_logits_
     nc = tc.nc
     with ExitStack() as ctx:
         const = ctx.enter_context(tc.tile_pool(name="const", bufs=1))
-        xin = ctx.enter_context(tc.tile_pool(name="xin", bufs=3))
+        xin = ctx.enter_context(tc.tile_pool(name="xin", bufs=CHUNKS))
         work = ctx.enter_context(tc.tile_pool(name="work", bufs=2))
         ostage = ctx.enter_context(tc.tile_pool(name="ostage", bufs=4))
         psum_stream = ctx.enter_context(tc.psum_pool(name="psum_stream", bufs=5))
@@ -56,29 +56,24 @@ def tile_treemodel_kernel(tc, x, W_gate, b_gate, leaf_logits_words, leaf_logits_
         nc.scalar.dma_start(out=b_src[32:34, 0:128], in_=b_gate[255:511].rearrange("(g m) -> g m", g=2))
         nc.scalar.dma_start(out=b_src[64:66, 0:64], in_=b_gate[127:255].rearrange("(g j) -> g j", g=2))
 
-        x_rows = {}
-
-        def x_load(n, pieces):
-            x_rows[n] = xin.tile([P, ROW_TILES, FEATURES], BF16, name="x_sb")
-            step = ROW_TILES // pieces
-            for i in range(pieces):
-                nc.sync.dma_start(
-                    out=x_rows[n][:, step * i : step * i + step, :], in_=x_chunks[n][:, step * i : step * i + step, :]
-                )
-
+        x_rows = []
+        for n in range(CHUNKS):
+            x_rows.append(xin.tile([P, ROW_TILES, FEATURES], BF16, name="x_sb"))
         w_raw = const.tile([P, 4, 2, 1024], BF16)
         w_rows = W_gate.rearrange("(a p e) c -> a p e c", a=4, p=P, e=2)
         w_top = const.tile([P, 4, 2, TOP], BF16)
         top_rows = W_gate.rearrange("(a p e) c -> e p a c", a=4, p=P, e=2)
-        x_load(0, 2)
+        nc.sync.dma_start(out=x_rows[0][:, 0:2, :], in_=x_chunks[0][:, 0:2, :])
         for e in range(2):
             nc.sync.dma_start(out=w_top[:, :, e, :], in_=top_rows[e][:, :, 0:TOP])
-        x_load(1, 1)
+        nc.sync.dma_start(out=x_rows[0][:, 2:4, :], in_=x_chunks[0][:, 2:4, :])
+        nc.sync.dma_start(out=x_rows[1][:], in_=x_chunks[1])
         for a in range(4):
             nc.sync.dma_start(out=w_raw[:, a, :, 0:1023], in_=w_rows[a])
         w_planes = w_raw[:].rearrange("p (g u) e c -> p g (u e) c", g=PASSES)
         top_planes = w_top[:].rearrange("p (g u) e c -> p g (u e) c", g=PASSES)
-        x_load(2, 1)
+        for n in range(2, CHUNKS):
+            nc.sync.dma_start(out=x_rows[n][:], in_=x_chunks[n])
 
         leaf_scales = const.tile([P, PASSES, CLASSES], U8, align_bytes=64)
         nc.vector.memset(leaf_scales[:].rearrange("p g n -> p (g n)").bitcast(I32), 0)
@@ -264,9 +259,9 @@ def tile_treemodel_kernel(tc, x, W_gate, b_gate, leaf_logits_words, leaf_logits_
             if slot == 0:
                 turn7 = work.tile([P, 2, CHUNK], F32)
                 right8 = work.tile([P, 2, CHUNK], F32)
-                turn9 = work.tile([P, 2, 4, CHUNK], F32)
-                low_of[n] = (turn7, right8, turn9)
-            turn7, right8, turn9 = low_of[n]
+                right9 = work.tile([P, 2, 2, CHUNK], F32)
+                low_of[n] = (turn7, right8, right9)
+            turn7, right8, right9 = low_of[n]
             z = low_logits(xq_of[n][0], xq_of[n][1], slot)
             if slot < 2:
                 nc.scalar.activation(
@@ -276,7 +271,7 @@ def tile_treemodel_kernel(tc, x, W_gate, b_gate, leaf_logits_words, leaf_logits_
                 nc.scalar.activation(out=right8[:, slot - 2, :], in_=z[:], func=SIGMOID, bias=column(32 + slot - 2))
             else:
                 c, g9 = divmod(slot - 4, 2)
-                nc.scalar.activation(out=turn9[:, g9, 2 * c + 1, :], in_=z[:], func=SIGMOID, bias=column(slot - 4))
+                nc.scalar.activation(out=right9[:, g9, c, :], in_=z[:], func=SIGMOID, bias=column(slot - 4))
 
         def reach7_transpose(n):
             reach7 = reach7_of[n]
@@ -292,47 +287,46 @@ def tile_treemodel_kernel(tc, x, W_gate, b_gate, leaf_logits_words, leaf_logits_
                 banks.append(pt)
             pt_of[n] = banks
 
-        reach8_of = {}
-        reach9_of = {}
+        minus8_of = {}
+        minus9_of = {}
         probs_of = {}
         pq_of = {}
 
         def reach8(n, g):
             if g == 0:
-                reach8_of[n] = work.tile([P, 2, CHUNK], F32, name="reach8", bufs=1)
-            nc.vector.tensor_tensor(out=reach8_of[n][:, g, :], in0=pt_of[n][g][:], in1=low_of[n][0][:, g, :], op=ALU.mult)
+                minus8_of[n] = work.tile([P, 2, CHUNK], F32, name="minus8")
+            nc.vector.scalar_tensor_tensor(
+                out=minus8_of[n][:, g, :], in0=pt_of[n][g][:], scalar=-1.0, in1=low_of[n][0][:, g, :],
+                op0=ALU.mult, op1=ALU.mult,
+            )
 
         def reach9_right(n):
-            reach9_of[n] = work.tile([P, 2, 2, CHUNK], F32, name="reach9", bufs=1)
-            nc.vector.tensor_tensor(out=reach9_of[n][:, :, 1, :], in0=reach8_of[n][:], in1=low_of[n][1][:], op=ALU.mult)
+            minus9_of[n] = work.tile([P, 2, 2, CHUNK], F32, name="minus9")
+            nc.vector.tensor_tensor(out=minus9_of[n][:, :, 1, :], in0=minus8_of[n][:], in1=low_of[n][1][:], op=ALU.mult)
 
         def reach9_left(n):
             nc.vector.tensor_tensor(
-                out=reach9_of[n][:, :, 0, :], in0=reach8_of[n][:], in1=reach9_of[n][:, :, 1, :], op=ALU.subtract
+                out=minus9_of[n][:, :, 0, :], in0=minus8_of[n][:], in1=minus9_of[n][:, :, 1, :], op=ALU.subtract
             )
+            probs_of[n] = work.tile([P, PASSES, CHUNK, 4], BF16, align_bytes=64, name="probs")
+            pc = work.tile([P, PASSES, CHUNK], U32, align_bytes=64)
+            ps = work.tile([P, PASSES, CHUNK], U8, align_bytes=64)
+            pq_of[n] = (pc, ps)
 
-        def left_turns(n, g):
-            both = low_of[n][2][:, g].rearrange("p (c e) b -> p c e b", e=2)
-            nc.vector.tensor_scalar(
-                out=both[:, :, 0, :], in0=both[:, :, 1, :], scalar1=-1.0, scalar2=1.0, op0=ALU.mult, op1=ALU.add
-            )
+        def leaf_probs(n, cols, g, e):
+            pairs = probs_of[n][:, g, cols, :].rearrange("p b (c e) -> p b c e", e=2)
+            turn_right = low_of[n][2][:, g, :, cols].rearrange("p c b -> p b c")
+            parent = minus9_of[n][:, g, :, cols].rearrange("p c b -> p b c")
+            if e == 1:
+                nc.vector.scalar_tensor_tensor(
+                    out=pairs[:, :, :, 1], in0=turn_right, scalar=-1.0, in1=parent, op0=ALU.mult, op1=ALU.mult
+                )
+            else:
+                nc.vector.scalar_tensor_tensor(
+                    out=pairs[:, :, :, 0], in0=turn_right, scalar=1.0, in1=parent, op0=ALU.subtract, op1=ALU.mult
+                )
 
-        def leaf_probs(n, h, g):
-            if h == 0 and g == 0:
-                probs_of[n] = work.tile([P, PASSES, CHUNK, 4], BF16, align_bytes=64, name="probs")
-                pc = work.tile([P, PASSES, CHUNK], U32, align_bytes=64)
-                ps = work.tile([P, PASSES, CHUNK], U8, align_bytes=64)
-                pq_of[n] = (pc, ps)
-            cols = slice(HALF * h, HALF * h + HALF)
-            nc.vector.tensor_tensor(
-                out=probs_of[n][:, g, cols, :].rearrange("p b (c e) -> p b c e", e=2),
-                in0=reach9_of[n][:, g, :, cols].rearrange("p c b -> p b c").unsqueeze(3).to_broadcast([P, HALF, 2, 2]),
-                in1=low_of[n][2][:, g, :, cols].rearrange("p (c e) b -> p b c e", e=2),
-                op=ALU.mult,
-            )
-
-        def leaf_quantise(n, h, g):
-            cols = slice(HALF * h, HALF * h + HALF)
+        def leaf_quantise(n, cols, g):
             pc, ps = pq_of[n]
             nc.vector.quantize_mx(
                 out=pc[:, g, cols].bitcast(FP8X4),
@@ -360,7 +354,10 @@ def tile_treemodel_kernel(tc, x, W_gate, b_gate, leaf_logits_words, leaf_logits_
                     stop=(g == PASSES - 1),
                 )
             nc.scalar.copy(out=rows_of[n][:, 512 * half : 512 * half + 512], in_=acc[:])
-            if half == 1:
+            if n == CHUNKS - 1 and q == ROW_TILES - 1:
+                cols = slice(512 * half, 512 * half + 512)
+                nc.sync.dma_start(out=out_tiles[n, q][:, cols], in_=rows_of[n][:, cols])
+            elif half == 1:
                 nc.sync.dma_start(out=out_tiles[n, q], in_=rows_of[n][:])
 
         def vector_period(n):
@@ -376,33 +373,32 @@ def tile_treemodel_kernel(tc, x, W_gate, b_gate, leaf_logits_words, leaf_logits_
             if live(n):
                 reach9_left(n)
             sweep_level(n + 1, 4)
-            if live(n):
-                left_turns(n, 0)
-            sweep_level(n + 1, 5)
-            if live(n):
-                left_turns(n, 1)
             x_quantise(n + 2, 0)
+            sweep_level(n + 1, 5)
             x_quantise(n + 2, 1)
-            for h in range(2):
+            pieces = 4 if n == CHUNKS - 1 else 2
+            width = CHUNK // pieces
+            for h in range(pieces):
+                cols = slice(width * h, width * h + width)
                 for g in range(PASSES):
-                    if h == 0:
-                        sweep_last(n + 1, 2 * g)
-                        sweep_last(n + 1, 2 * g + 1)
-                    if live(n):
-                        leaf_probs(n, h, g)
+                    for e in range(2):
+                        if h == 0:
+                            sweep_last(n + 1, 2 * g + e)
+                        if live(n):
+                            leaf_probs(n, cols, g, e)
                 if live(n):
                     for g in range(PASSES):
-                        leaf_quantise(n, h, g)
+                        leaf_quantise(n, cols, g)
 
         def front(n_x, n_top):
             for q in range(ROW_TILES):
-                x_transpose(n_x, q // 2, q % 2)
                 top_logits(n_top, q)
             top_turns(n_top)
+            for q in range(ROW_TILES):
+                x_transpose(n_x, q // 2, q % 2)
 
         front(0, -1)
         spread_bias()
-        x_load(3, 1)
         front(1, 0)
         x_quantise(0, 0)
         x_quantise(0, 1)
@@ -417,9 +413,13 @@ def tile_treemodel_kernel(tc, x, W_gate, b_gate, leaf_logits_words, leaf_logits_
             if n == -1:
                 for g in range(PASSES):
                     quantise_w(g, 512)
-            front(n + 3, n + 2)
+                front(-1, 1)
+            else:
+                front(n + 3, n + 2)
             for i in range(SLOTS):
                 leaves(n - 1, i // 2, i % 2)
                 low_turn(n + 1, i)
                 if i == 3 and live(n + 1):
                     reach7_transpose(n + 1)
+                    if n == -1:
+                        front(2, -1)

@@ -33,6 +33,7 @@ def tile_treemodel_kernel(tc, x, W_gate, b_gate, leaf_logits_words, leaf_logits_
         const = ctx.enter_context(tc.tile_pool(name="const", bufs=1))
         xin = ctx.enter_context(tc.tile_pool(name="xin", bufs=CHUNKS))
         work = ctx.enter_context(tc.tile_pool(name="work", bufs=2))
+        turns = ctx.enter_context(tc.tile_pool(name="turns", bufs=2))
         ostage = ctx.enter_context(tc.tile_pool(name="ostage", bufs=4))
         psum_stream = ctx.enter_context(tc.psum_pool(name="psum_stream", bufs=5))
         psum_top = ctx.enter_context(tc.psum_pool(name="psum_top", bufs=1))
@@ -59,7 +60,7 @@ def tile_treemodel_kernel(tc, x, W_gate, b_gate, leaf_logits_words, leaf_logits_
         x_rows = []
         for n in range(CHUNKS):
             x_rows.append(xin.tile([P, ROW_TILES, FEATURES], BF16, name="x_sb"))
-        w_raw = const.tile([P, 4, 2, 1024], BF16)
+        w_raw = turns.tile([P, 4, 2, 1024], BF16, align_bytes=64, name="turn9")
         w_rows = W_gate.rearrange("(a p e) c -> a p e c", a=4, p=P, e=2)
         w_top = const.tile([P, 4, 2, TOP], BF16)
         top_rows = W_gate.rearrange("(a p e) c -> e p a c", a=4, p=P, e=2)
@@ -105,16 +106,18 @@ def tile_treemodel_kernel(tc, x, W_gate, b_gate, leaf_logits_words, leaf_logits_
         nc.vector.memset(b_pairs[96:128, :, 1], 1.0)
         nc.vector.memset(b_pairs[96:128, :, 0], -1.0)
         bias_cols = const.tile([P, P], F32)
+        bias_minus = const.tile([P, P], F32)
 
         def spread_bias():
             b_ps = psum_pt.tile([P, P], F32, name="pt")
             nc.tensor.transpose(out=b_ps[:], in_=b_all[:], identity=ident[:])
             nc.vector.tensor_copy(out=bias_cols[:], in_=b_ps[:])
+            nc.vector.tensor_scalar_mul(out=bias_minus[:], in0=bias_cols[:], scalar1=-1.0)
 
         def column(i):
             return bias_cols[:, i : i + 1]
 
-        wg = const.tile([P, PASSES, SLOTS * P, 4], BF16, align_bytes=64)
+        wg = turns.tile([P, PASSES, SLOTS * P, 4], BF16, align_bytes=64, name="turn9")
         wc = const.tile([P, PASSES, SLOTS * P], U32, align_bytes=64)
         ws = const.tile([P, PASSES, SLOTS * P], U8, align_bytes=64)
 
@@ -259,9 +262,9 @@ def tile_treemodel_kernel(tc, x, W_gate, b_gate, leaf_logits_words, leaf_logits_
             if slot == 0:
                 turn7 = work.tile([P, 2, CHUNK], F32)
                 right8 = work.tile([P, 2, CHUNK], F32)
-                right9 = work.tile([P, 2, 2, CHUNK], F32)
-                low_of[n] = (turn7, right8, right9)
-            turn7, right8, right9 = low_of[n]
+                turn9 = turns.tile([P, 2, 2, 2, CHUNK], F32, align_bytes=64, name="turn9")
+                low_of[n] = (turn7, right8, turn9)
+            turn7, right8, turn9 = low_of[n]
             z = low_logits(xq_of[n][0], xq_of[n][1], slot)
             if slot < 2:
                 nc.scalar.activation(
@@ -271,7 +274,12 @@ def tile_treemodel_kernel(tc, x, W_gate, b_gate, leaf_logits_words, leaf_logits_
                 nc.scalar.activation(out=right8[:, slot - 2, :], in_=z[:], func=SIGMOID, bias=column(32 + slot - 2))
             else:
                 c, g9 = divmod(slot - 4, 2)
-                nc.scalar.activation(out=right9[:, g9, c, :], in_=z[:], func=SIGMOID, bias=column(slot - 4))
+                nc.scalar.activation(out=turn9[:, g9, c, 1, :], in_=z[:], func=SIGMOID, bias=column(slot - 4))
+                if g9 == 0:
+                    nc.scalar.activation(
+                        out=turn9[:, g9, c, 0, :], in_=z[:], func=SIGMOID, scale=-1.0,
+                        bias=bias_minus[:, slot - 4 : slot - 3],
+                    )
 
         def reach7_transpose(n):
             reach7 = reach7_of[n]
@@ -287,44 +295,52 @@ def tile_treemodel_kernel(tc, x, W_gate, b_gate, leaf_logits_words, leaf_logits_
                 banks.append(pt)
             pt_of[n] = banks
 
-        minus8_of = {}
-        minus9_of = {}
+        reach8_of = {}
+        reach9_of = {}
         probs_of = {}
         pq_of = {}
 
         def reach8(n, g):
             if g == 0:
-                minus8_of[n] = work.tile([P, 2, CHUNK], F32, name="minus8")
-            nc.vector.scalar_tensor_tensor(
-                out=minus8_of[n][:, g, :], in0=pt_of[n][g][:], scalar=-1.0, in1=low_of[n][0][:, g, :],
-                op0=ALU.mult, op1=ALU.mult,
+                reach8_of[n] = work.tile([P, 2, CHUNK], F32, name="reach8")
+            nc.vector.tensor_tensor(
+                out=reach8_of[n][:, g, :], in0=pt_of[n][g][:], in1=low_of[n][0][:, g, :], op=ALU.mult
             )
 
+        def child9(n, c):
+            return reach9_of[n][:].rearrange("p g h c i -> p (g h) c i")[:, :, c, :]
+
+        def by_four(ap):
+            return ap.rearrange("p g (h i) -> p (g h) i", i=4)
+
         def reach9_right(n):
-            minus9_of[n] = work.tile([P, 2, 2, CHUNK], F32, name="minus9")
-            nc.vector.tensor_tensor(out=minus9_of[n][:, :, 1, :], in0=minus8_of[n][:], in1=low_of[n][1][:], op=ALU.mult)
+            reach9_of[n] = work.tile([P, 2, CHUNK // 4, 2, 4], F32, align_bytes=64, name="reach9")
+            nc.vector.tensor_tensor(
+                out=child9(n, 1), in0=by_four(reach8_of[n][:]), in1=by_four(low_of[n][1][:]), op=ALU.mult
+            )
 
         def reach9_left(n):
             nc.vector.tensor_tensor(
-                out=minus9_of[n][:, :, 0, :], in0=minus8_of[n][:], in1=minus9_of[n][:, :, 1, :], op=ALU.subtract
+                out=child9(n, 0), in0=by_four(reach8_of[n][:]), in1=child9(n, 1), op=ALU.subtract
             )
             probs_of[n] = work.tile([P, PASSES, CHUNK, 4], BF16, align_bytes=64, name="probs")
             pc = work.tile([P, PASSES, CHUNK], U32, align_bytes=64)
             ps = work.tile([P, PASSES, CHUNK], U8, align_bytes=64)
             pq_of[n] = (pc, ps)
 
-        def leaf_probs(n, cols, g, e):
-            pairs = probs_of[n][:, g, cols, :].rearrange("p b (c e) -> p b c e", e=2)
-            turn_right = low_of[n][2][:, g, :, cols].rearrange("p c b -> p b c")
-            parent = minus9_of[n][:, g, :, cols].rearrange("p c b -> p b c")
-            if e == 1:
-                nc.vector.scalar_tensor_tensor(
-                    out=pairs[:, :, :, 1], in0=turn_right, scalar=-1.0, in1=parent, op0=ALU.mult, op1=ALU.mult
-                )
-            else:
-                nc.vector.scalar_tensor_tensor(
-                    out=pairs[:, :, :, 0], in0=turn_right, scalar=1.0, in1=parent, op0=ALU.subtract, op1=ALU.mult
-                )
+        def turn9_left(n):
+            turn9 = low_of[n][2]
+            nc.vector.tensor_scalar(
+                out=turn9[:, 1, :, 0, :], in0=turn9[:, 1, :, 1, :], scalar1=-1.0, scalar2=1.0,
+                op0=ALU.mult, op1=ALU.add,
+            )
+
+        def leaf_probs(n, first, width, g):
+            fours = slice(first // 4, (first + width) // 4)
+            parent = reach9_of[n][:, g, fours, :, :].unsqueeze(3).to_broadcast([P, width // 4, 2, 2, 4])
+            turn = low_of[n][2][:, g, :, :, first : first + width].rearrange("p c e (h i) -> p h c e i", i=4)
+            leaf = probs_of[n][:, g, first : first + width, :].rearrange("p (h i) (c e) -> p h c e i", i=4, e=2)
+            nc.vector.tensor_tensor(out=leaf, in0=parent, in1=turn, op=ALU.mult)
 
         def leaf_quantise(n, cols, g):
             pc, ps = pq_of[n]
@@ -371,6 +387,7 @@ def tile_treemodel_kernel(tc, x, W_gate, b_gate, leaf_logits_words, leaf_logits_
                 reach9_right(n)
             sweep_level(n + 1, 3)
             if live(n):
+                turn9_left(n)
                 reach9_left(n)
             sweep_level(n + 1, 4)
             x_quantise(n + 2, 0)
@@ -381,11 +398,11 @@ def tile_treemodel_kernel(tc, x, W_gate, b_gate, leaf_logits_words, leaf_logits_
             for h in range(pieces):
                 cols = slice(width * h, width * h + width)
                 for g in range(PASSES):
-                    for e in range(2):
-                        if h == 0:
+                    if h == 0:
+                        for e in range(2):
                             sweep_last(n + 1, 2 * g + e)
-                        if live(n):
-                            leaf_probs(n, cols, g, e)
+                    if live(n):
+                        leaf_probs(n, width * h, width, g)
                 if live(n):
                     for g in range(PASSES):
                         leaf_quantise(n, cols, g)

@@ -33,6 +33,7 @@ def tile_treemodel_kernel(tc, x, W_gate, b_gate, leaf_logits_words, leaf_logits_
         const = ctx.enter_context(tc.tile_pool(name="const", bufs=1))
         xin = ctx.enter_context(tc.tile_pool(name="xin", bufs=CHUNKS))
         work = ctx.enter_context(tc.tile_pool(name="work", bufs=2))
+        xqp = ctx.enter_context(tc.tile_pool(name="xqp", bufs=3))
         turns = ctx.enter_context(tc.tile_pool(name="turns", bufs=2))
         ostage = ctx.enter_context(tc.tile_pool(name="ostage", bufs=4))
         psum_stream = ctx.enter_context(tc.psum_pool(name="psum_stream", bufs=5))
@@ -45,6 +46,9 @@ def tile_treemodel_kernel(tc, x, W_gate, b_gate, leaf_logits_words, leaf_logits_
 
         def live(n):
             return 0 <= n < CHUNKS
+
+        def pieces_of(n):
+            return 4 if n == CHUNKS - 1 else 2
 
         bias_row = const.tile([P, TOP], BF16)
         nc.vector.memset(bias_row[:], 0.0)
@@ -131,8 +135,8 @@ def tile_treemodel_kernel(tc, x, W_gate, b_gate, leaf_logits_words, leaf_logits_
                 in_=w_planes[:, g, :, 255:511].rearrange("p t j -> p j t"),
             )
 
-        def regroup_level_9(g):
-            nc.scalar.copy(
+        def regroup_level_9(copy, g):
+            copy(
                 out=wg[:, g, 512:1024, :].rearrange("p (c j) t -> p c j t", c=2),
                 in_=w_planes[:, g, :, 511:1023].rearrange("p t (j c) -> p c j t", c=2),
             )
@@ -164,18 +168,16 @@ def tile_treemodel_kernel(tc, x, W_gate, b_gate, leaf_logits_words, leaf_logits_
             dst = xg_of[n][:, g, HALF * h : HALF * h + HALF, :].rearrange("p b t -> p (b t)").bitcast(F32)
             nc.scalar.copy(out=dst.rearrange("p (b u) -> p b u", u=2), in_=xt[:].rearrange("p u b -> p b u"))
 
-        def x_quantise(n, g):
+        def x_quantise(n):
             if not live(n):
                 return
-            if g == 0:
-                xc = work.tile([P, PASSES, CHUNK], U32, align_bytes=64)
-                xs = work.tile([P, PASSES, CHUNK], U8, align_bytes=64)
-                xq_of[n] = (xc, xs)
-            xc, xs = xq_of[n]
+            xc = xqp.tile([P, PASSES, CHUNK], U32, align_bytes=64)
+            xs = xqp.tile([P, PASSES, CHUNK], U8, align_bytes=64)
+            xq_of[n] = (xc, xs)
             nc.vector.quantize_mx(
-                out=xc[:, g, :].bitcast(FP8X4),
-                scales=xs[:, g, :],
-                in_=xg_of[n][:, g].rearrange("p b t -> p (b t)"),
+                out=xc[:].rearrange("p g b -> p (g b)").bitcast(FP8X4),
+                scales=xs[:].rearrange("p g b -> p (g b)"),
+                in_=xg_of[n][:].rearrange("p g b t -> p (g b t)"),
             )
 
         turn_of = {}
@@ -202,42 +204,46 @@ def tile_treemodel_kernel(tc, x, W_gate, b_gate, leaf_logits_words, leaf_logits_
         def top_turns(n):
             if not live(n):
                 return
-            turn = work.tile([P, 2, ROW_TILES, TOP], F32)
-            nc.scalar.activation(out=turn[:, 1], in_=top_of[n][:], func=SIGMOID)
-            nc.scalar.activation(out=turn[:, 0], in_=top_of[n][:], func=SIGMOID, scale=-1.0)
-            turn_of[n] = turn
+            low = work.tile([P, 2, ROW_TILES, 64], F32, name="turn_low")
+            six = work.tile([P, 2, ROW_TILES, 64], F32, name="turn_six")
+            for c, scale in ((1, 1.0), (0, -1.0)):
+                nc.scalar.activation(out=low[:, c, :, 0:63], in_=top_of[n][:, :, 0:63], func=SIGMOID, scale=scale)
+            for c, scale in ((1, 1.0), (0, -1.0)):
+                nc.scalar.activation(out=six[:, c], in_=top_of[n][:, :, 63:127], func=SIGMOID, scale=scale)
+            turn_of[n] = (low, six)
 
         reach_of = {}
 
         def sweep_level(n, level):
             if not live(n):
                 return
-            turn = turn_of[n]
+            low = turn_of[n][0]
             nodes = 2**level
             if level == 1:
-                reach = turn[:, :, :, 0].rearrange("p j q -> p q j")
+                reach = low[:, :, :, 0].rearrange("p c q -> p q c")
             else:
                 reach = reach_of[n][:]
             children = work.tile([P, ROW_TILES, 2 * nodes], F32, name="reach%d" % (level + 1))
             nc.vector.tensor_tensor(
                 out=children[:].rearrange("p q (j c) -> p q j c", c=2),
                 in0=reach.unsqueeze(3).to_broadcast([P, ROW_TILES, nodes, 2]),
-                in1=turn[:, :, :, nodes - 1 : 2 * nodes - 1].rearrange("p c q j -> p q j c"),
+                in1=low[:, :, :, nodes - 1 : 2 * nodes - 1].rearrange("p c q j -> p q j c"),
                 op=ALU.mult,
             )
             reach_of[n] = children
 
-        def sweep_last(n, q):
+        def sweep_last(n):
             if not live(n):
                 return
-            if q == 0:
-                reach7_of[n] = work.tile([P, ROW_TILES, 256], F32, name="reach7")
+            reach7 = work.tile([P, ROW_TILES, 256], F32, name="reach7")
+            shape = [P, ROW_TILES * 64, 2, 2]
             nc.vector.tensor_tensor(
-                out=reach7_of[n][:, q, :].rearrange("p (j c d) -> p j c d", c=2, d=2),
-                in0=reach_of[n][:, q, :].unsqueeze(2).unsqueeze(3).to_broadcast([P, 64, 2, 2]),
-                in1=turn_of[n][:, :, q, 63:127].rearrange("p c j -> p j c").unsqueeze(3).to_broadcast([P, 64, 2, 2]),
+                out=reach7[:].rearrange("p q (j c d) -> p (q j) c d", c=2, d=2),
+                in0=reach_of[n][:].rearrange("p q j -> p (q j)").unsqueeze(2).unsqueeze(3).to_broadcast(shape),
+                in1=turn_of[n][1][:].rearrange("p c q j -> p (q j) c").unsqueeze(3).to_broadcast(shape),
                 op=ALU.mult,
             )
+            reach7_of[n] = reach7
 
         low_of = {}
         pt_of = {}
@@ -259,29 +265,38 @@ def tile_treemodel_kernel(tc, x, W_gate, b_gate, leaf_logits_words, leaf_logits_
         def low_turn(n, slot):
             if not live(n):
                 return
+            pieces = pieces_of(n)
+            width = CHUNK // pieces
             if slot == 0:
                 turn7 = work.tile([P, 2, CHUNK], F32)
-                right8 = work.tile([P, 2, CHUNK], F32)
-                turn9 = turns.tile([P, 2, 2, 2, CHUNK], F32, align_bytes=64, name="turn9")
+                right8 = work.tile([P, pieces, 2, width], F32)
+                turn9 = turns.tile([P, pieces, 2, 2, 2, width], F32, align_bytes=64, name="turn9")
                 low_of[n] = (turn7, right8, turn9)
             turn7, right8, turn9 = low_of[n]
             z = low_logits(xq_of[n][0], xq_of[n][1], slot)
+            z_pieces = z[:].rearrange("p (h b) -> p h b", h=pieces)
             if slot < 2:
                 nc.scalar.activation(
                     out=turn7[:, slot, :], in_=z[:], func=SIGMOID, bias=column(64 + slot), scale=column(96)
                 )
             elif slot < 4:
-                nc.scalar.activation(out=right8[:, slot - 2, :], in_=z[:], func=SIGMOID, bias=column(32 + slot - 2))
+                nc.scalar.activation(
+                    out=right8[:, :, slot - 2, :], in_=z_pieces, func=SIGMOID, bias=column(32 + slot - 2)
+                )
             else:
                 c, g9 = divmod(slot - 4, 2)
-                nc.scalar.activation(out=turn9[:, g9, c, 1, :], in_=z[:], func=SIGMOID, bias=column(slot - 4))
-                if g9 == 0:
+                nc.scalar.activation(
+                    out=turn9[:, :, c, 1, g9, :], in_=z_pieces, func=SIGMOID, bias=column(slot - 4)
+                )
+                if c == 1:
                     nc.scalar.activation(
-                        out=turn9[:, g9, c, 0, :], in_=z[:], func=SIGMOID, scale=-1.0,
+                        out=turn9[:, :, c, 0, g9, :], in_=z_pieces, func=SIGMOID, scale=-1.0,
                         bias=bias_minus[:, slot - 4 : slot - 3],
                     )
 
         def reach7_transpose(n):
+            if not live(n):
+                return
             reach7 = reach7_of[n]
             banks = []
             for g in range(2):
@@ -301,53 +316,79 @@ def tile_treemodel_kernel(tc, x, W_gate, b_gate, leaf_logits_words, leaf_logits_
         pq_of = {}
 
         def reach8(n, g):
+            if not live(n):
+                return
+            pieces = pieces_of(n)
             if g == 0:
-                reach8_of[n] = work.tile([P, 2, CHUNK], F32, name="reach8")
+                reach8_of[n] = work.tile([P, pieces, 2, CHUNK // pieces], F32, name="reach8")
             nc.vector.tensor_tensor(
-                out=reach8_of[n][:, g, :], in0=pt_of[n][g][:], in1=low_of[n][0][:, g, :], op=ALU.mult
+                out=reach8_of[n][:, :, g, :],
+                in0=pt_of[n][g][:].rearrange("p (h b) -> p h b", h=pieces),
+                in1=low_of[n][0][:, g, :].rearrange("p (h b) -> p h b", h=pieces),
+                op=ALU.mult,
             )
-
-        def child9(n, c):
-            return reach9_of[n][:].rearrange("p g h c i -> p (g h) c i")[:, :, c, :]
 
         def by_four(ap):
-            return ap.rearrange("p g (h i) -> p (g h) i", i=4)
+            return ap.rearrange("p h g b -> p (h g b)").rearrange("p (k i) -> p k i", i=4)
 
-        def reach9_right(n):
-            reach9_of[n] = work.tile([P, 2, CHUNK // 4, 2, 4], F32, align_bytes=64, name="reach9")
-            nc.vector.tensor_tensor(
-                out=child9(n, 1), in0=by_four(reach8_of[n][:]), in1=by_four(low_of[n][1][:]), op=ALU.mult
-            )
+        def child9(n, c):
+            return reach9_of[n][:].rearrange("p h g k c i -> p (h g k) c i")[:, :, c, :]
 
-        def reach9_left(n):
-            nc.vector.tensor_tensor(
-                out=child9(n, 0), in0=by_four(reach8_of[n][:]), in1=child9(n, 1), op=ALU.subtract
-            )
-            probs_of[n] = work.tile([P, PASSES, CHUNK, 4], BF16, align_bytes=64, name="probs")
-            pc = work.tile([P, PASSES, CHUNK], U32, align_bytes=64)
-            ps = work.tile([P, PASSES, CHUNK], U8, align_bytes=64)
-            pq_of[n] = (pc, ps)
+        def reach9(n, c):
+            if not live(n):
+                return
+            pieces = pieces_of(n)
+            if c == 1:
+                reach9_of[n] = work.tile(
+                    [P, pieces, 2, CHUNK // pieces // 4, 2, 4], F32, align_bytes=64, name="reach9"
+                )
+                nc.vector.tensor_tensor(
+                    out=child9(n, 1), in0=by_four(reach8_of[n][:]), in1=by_four(low_of[n][1][:]), op=ALU.mult
+                )
+            else:
+                nc.vector.tensor_tensor(
+                    out=child9(n, 0), in0=by_four(reach8_of[n][:]), in1=child9(n, 1), op=ALU.subtract
+                )
 
         def turn9_left(n):
+            if not live(n):
+                return
             turn9 = low_of[n][2]
             nc.vector.tensor_scalar(
-                out=turn9[:, 1, :, 0, :], in0=turn9[:, 1, :, 1, :], scalar1=-1.0, scalar2=1.0,
-                op0=ALU.mult, op1=ALU.add,
+                out=turn9[:, :, 0, 0].rearrange("p h g b -> p h (g b)"),
+                in0=turn9[:, :, 0, 1].rearrange("p h g b -> p h (g b)"),
+                scalar1=-1.0, scalar2=1.0, op0=ALU.mult, op1=ALU.add,
             )
 
-        def leaf_probs(n, first, width, g):
-            fours = slice(first // 4, (first + width) // 4)
-            parent = reach9_of[n][:, g, fours, :, :].unsqueeze(3).to_broadcast([P, width // 4, 2, 2, 4])
-            turn = low_of[n][2][:, g, :, :, first : first + width].rearrange("p c e (h i) -> p h c e i", i=4)
-            leaf = probs_of[n][:, g, first : first + width, :].rearrange("p (h i) (c e) -> p h c e i", i=4, e=2)
-            nc.vector.tensor_tensor(out=leaf, in0=parent, in1=turn, op=ALU.mult)
+        def leaf_probs(n, h):
+            if not live(n):
+                return
+            pieces = pieces_of(n)
+            width = CHUNK // pieces
+            if h == 0:
+                probs_of[n] = work.tile([P, pieces, PASSES, width, 4], BF16, align_bytes=64, name="probs")
+                pc = work.tile([P, pieces, PASSES, width], U32, align_bytes=64)
+                ps = work.tile([P, pieces, PASSES, width], U8, align_bytes=64)
+                pq_of[n] = (pc, ps)
+            fours = PASSES * width // 4
+            parent = reach9_of[n][:, h].rearrange("p g k c i -> p (g k) c i")
+            turn = low_of[n][2][:, h].rearrange("p c e g b -> p c e (g b)")
+            leaf = probs_of[n][:, h].rearrange("p g b t -> p (g b) t")
+            nc.vector.tensor_tensor(
+                out=leaf.rearrange("p (k i) (c e) -> p k c e i", i=4, e=2),
+                in0=parent.unsqueeze(3).to_broadcast([P, fours, 2, 2, 4]),
+                in1=turn.rearrange("p c e (k i) -> p k c e i", i=4),
+                op=ALU.mult,
+            )
 
-        def leaf_quantise(n, cols, g):
+        def leaf_quantise(n, h):
+            if not live(n):
+                return
             pc, ps = pq_of[n]
             nc.vector.quantize_mx(
-                out=pc[:, g, cols].bitcast(FP8X4),
-                scales=ps[:, g, cols],
-                in_=probs_of[n][:, g, cols, :].rearrange("p b t -> p (b t)"),
+                out=pc[:, h].rearrange("p g b -> p (g b)").bitcast(FP8X4),
+                scales=ps[:, h].rearrange("p g b -> p (g b)"),
+                in_=probs_of[n][:, h].rearrange("p g b t -> p (g b t)"),
             )
 
         rows_of = {}
@@ -356,87 +397,90 @@ def tile_treemodel_kernel(tc, x, W_gate, b_gate, leaf_logits_words, leaf_logits_
             if not live(n):
                 return
             pc, ps = pq_of[n]
+            h, first = divmod(P * q, CHUNK // pieces_of(n))
             if half == 0:
                 rows_of[n] = ostage.tile([P, CLASSES], F32, name="rows")
             acc = psum_stream.tile([P, 512], F32, name="stream")
             for g in range(PASSES):
                 nc.tensor.matmul_mx(
                     out=acc[:],
-                    lhsT=pc[:, g, P * q : P * q + P].bitcast(FP8X4),
-                    lhsT_scale=ps[:, g, P * q : P * q + P],
+                    lhsT=pc[:, h, g, first : first + P].bitcast(FP8X4),
+                    lhsT_scale=ps[:, h, g, first : first + P],
                     rhs=leaf_words[:, g, 2048 * half : 2048 * half + 2048].bitcast(FP8X4),
                     rhs_scale=leaf_scales[:, g, 512 * half : 512 * half + 512],
                     start=(g == 0),
                     stop=(g == PASSES - 1),
                 )
-            nc.scalar.copy(out=rows_of[n][:, 512 * half : 512 * half + 512], in_=acc[:])
-            if n == CHUNKS - 1 and q == ROW_TILES - 1:
-                cols = slice(512 * half, 512 * half + 512)
+            last = n == CHUNKS - 1 and q == ROW_TILES - 1
+            cols = slice(512 * half, 512 * half + 512)
+            copy = nc.vector.tensor_copy if last and half == 1 else nc.scalar.copy
+            copy(out=rows_of[n][:, cols], in_=acc[:])
+            if last:
                 nc.sync.dma_start(out=out_tiles[n, q][:, cols], in_=rows_of[n][:, cols])
             elif half == 1:
                 nc.sync.dma_start(out=out_tiles[n, q], in_=rows_of[n][:])
 
         def vector_period(n):
-            if live(n):
-                reach8(n, 0)
-            sweep_level(n + 1, 1)
-            if live(n):
-                reach8(n, 1)
-            sweep_level(n + 1, 2)
-            if live(n):
-                reach9_right(n)
-            sweep_level(n + 1, 3)
-            if live(n):
-                turn9_left(n)
-                reach9_left(n)
-            sweep_level(n + 1, 4)
-            x_quantise(n + 2, 0)
-            sweep_level(n + 1, 5)
-            x_quantise(n + 2, 1)
-            pieces = 4 if n == CHUNKS - 1 else 2
-            width = CHUNK // pieces
-            for h in range(pieces):
-                cols = slice(width * h, width * h + width)
-                for g in range(PASSES):
-                    if h == 0:
-                        for e in range(2):
-                            sweep_last(n + 1, 2 * g + e)
-                    if live(n):
-                        leaf_probs(n, width * h, width, g)
-                if live(n):
-                    for g in range(PASSES):
-                        leaf_quantise(n, cols, g)
+            turn9_left(n)
+            sweep_level(n + 2, 1)
+            leaf_probs(n, 0)
+            sweep_level(n + 2, 2)
+            reach8(n + 1, 0)
+            sweep_level(n + 2, 3)
+            reach8(n + 1, 1)
+            leaf_quantise(n, 0)
+            sweep_level(n + 2, 4)
+            reach9(n + 1, 1)
+            leaf_probs(n, 1)
+            sweep_level(n + 2, 5)
+            reach9(n + 1, 0)
+            if pieces_of(n) == 4:
+                leaf_probs(n, 2)
+            leaf_quantise(n, 1)
+            if pieces_of(n) == 4:
+                leaf_probs(n, 3)
+                leaf_quantise(n, 2)
+                leaf_quantise(n, 3)
+            x_quantise(n + 3)
+            sweep_last(n + 2)
 
-        def front(n_x, n_top):
+        def front(n):
             for q in range(ROW_TILES):
-                top_logits(n_top, q)
-            top_turns(n_top)
+                top_logits(n, q)
+            top_turns(n)
             for q in range(ROW_TILES):
-                x_transpose(n_x, q // 2, q % 2)
+                x_transpose(n + 1, q // 2, q % 2)
 
-        front(0, -1)
+        def late(n):
+            for i in range(4):
+                leaves(n - 1, 2 + i // 2, i % 2)
+                low_turn(n + 1, 4 + i)
+
+        def early(n):
+            for i in range(4):
+                leaves(n, i // 2, i % 2)
+                low_turn(n + 2, i)
+            reach7_transpose(n + 2)
+
+        def tensor_period(n):
+            late(n)
+            front(n + 3)
+            early(n)
+
+        tensor_period(-4)
         spread_bias()
-        front(1, 0)
-        x_quantise(0, 0)
-        x_quantise(0, 1)
-        for g in range(PASSES):
-            regroup_levels_7_8(g)
+        vector_period(-3)
+        tensor_period(-3)
+        regroup_levels_7_8(0)
+        regroup_level_9(nc.vector.tensor_copy, 0)
+        regroup_level_9(nc.scalar.copy, 1)
+        regroup_levels_7_8(1)
         for g in range(PASSES):
             quantise_w(g, 0)
+        vector_period(-2)
         for g in range(PASSES):
-            regroup_level_9(g)
-        for n in range(-1, CHUNKS + 1):
-            vector_period(n)
-            if n == -1:
-                for g in range(PASSES):
-                    quantise_w(g, 512)
-                front(-1, 1)
-            else:
-                front(n + 3, n + 2)
-            for i in range(SLOTS):
-                leaves(n - 1, i // 2, i % 2)
-                low_turn(n + 1, i)
-                if i == 3 and live(n + 1):
-                    reach7_transpose(n + 1)
-                    if n == -1:
-                        front(2, -1)
+            quantise_w(g, 512)
+        for n in range(-2, CHUNKS + 1):
+            if n > -2:
+                vector_period(n)
+            tensor_period(n)

@@ -22,7 +22,8 @@ HALF = CHUNK // 2
 ROW_TILES = CHUNK // P
 CHUNKS = BATCH // CHUNK
 TOP = 128
-SLOTS = 8
+UPPER = 384
+LAST = 512
 
 FLOPS = 2 * BATCH * FEATURES * (TOP + 896) + 2 * BATCH * 1024 * CLASSES
 
@@ -59,7 +60,7 @@ def tile_treemodel_kernel(tc, x, W_gate, b_gate, leaf_logits_words, leaf_logits_
         for c in range(2):
             nc.scalar.dma_start(out=b_src[2 * c : 2 * c + 2, 0:255], in_=level9_bias[:, c : c + 255])
         nc.scalar.dma_start(out=b_src[32:34, 0:128], in_=b_gate[255:511].rearrange("(g m) -> g m", g=2))
-        nc.scalar.dma_start(out=b_src[64:66, 0:64], in_=b_gate[127:255].rearrange("(g j) -> g j", g=2))
+        nc.scalar.dma_start(out=b_src[64:65, 0:128], in_=b_gate[127:255].rearrange("(o m) -> o m", o=1))
 
         x_rows = []
         for n in range(CHUNKS):
@@ -72,8 +73,10 @@ def tile_treemodel_kernel(tc, x, W_gate, b_gate, leaf_logits_words, leaf_logits_
         for e in range(2):
             nc.sync.dma_start(out=w_top[:, :, e, :], in_=top_rows[e][:, :, 0:TOP])
         nc.sync.dma_start(out=x_rows[0][:, 2:4, :], in_=x_chunks[0][:, 2:4, :])
+        for a in range(2):
+            nc.sync.dma_start(out=w_raw[:, a, :, 0:1023], in_=w_rows[a])
         nc.sync.dma_start(out=x_rows[1][:], in_=x_chunks[1])
-        for a in range(4):
+        for a in range(2, 4):
             nc.sync.dma_start(out=w_raw[:, a, :, 0:1023], in_=w_rows[a])
         w_planes = w_raw[:].rearrange("p (g u) e c -> p g (u e) c", g=PASSES)
         top_planes = w_top[:].rearrange("p (g u) e c -> p g (u e) c", g=PASSES)
@@ -104,11 +107,7 @@ def tile_treemodel_kernel(tc, x, W_gate, b_gate, leaf_logits_words, leaf_logits_
         b_all = const.tile([P, P], F32)
         nc.vector.tensor_copy(out=b_all[0:32, :], in_=b_src[0:32, 0:256:2])
         nc.vector.tensor_copy(out=b_all[32:64, :], in_=b_src[32:64, 0:128])
-        b_pairs = b_all[:].rearrange("p (j d) -> p j d", d=2)
-        nc.vector.tensor_copy(out=b_pairs[64:96, :, 1], in_=b_src[64:96, 0:64])
-        nc.vector.tensor_scalar_mul(out=b_pairs[64:96, :, 0], in0=b_src[64:96, 0:64], scalar1=-1.0)
-        nc.vector.memset(b_pairs[96:128, :, 1], 1.0)
-        nc.vector.memset(b_pairs[96:128, :, 0], -1.0)
+        nc.vector.tensor_copy(out=b_all[64:128, :], in_=b_src[64:128, 0:128])
         bias_cols = const.tile([P, P], F32)
         bias_minus = const.tile([P, P], F32)
 
@@ -121,32 +120,32 @@ def tile_treemodel_kernel(tc, x, W_gate, b_gate, leaf_logits_words, leaf_logits_
         def column(i):
             return bias_cols[:, i : i + 1]
 
-        wg = turns.tile([P, PASSES, SLOTS * P, 4], BF16, align_bytes=64, name="turn9")
-        wc = const.tile([P, PASSES, SLOTS * P], U32, align_bytes=64)
-        ws = const.tile([P, PASSES, SLOTS * P], U8, align_bytes=64)
+        w_halves = turns.tile([P, PASSES * (UPPER + LAST), 4], BF16, align_bytes=64, name="turn9")
+        wg_upper = w_halves[:, 0 : PASSES * UPPER, :].rearrange("p (g n) t -> p g n t", g=PASSES)
+        wg_last = w_halves[:, PASSES * UPPER :, :].rearrange("p (g n) t -> p g n t", g=PASSES)
+        wc = const.tile([P, PASSES * (UPPER + LAST)], U32, align_bytes=64)
+        ws = const.tile([P, PASSES * (UPPER + LAST)], U8, align_bytes=64)
 
         def regroup_levels_7_8(g):
-            nc.vector.tensor_copy(
-                out=wg[:, g, 0:256, :].rearrange("p (j d) t -> p j d t", d=2),
-                in_=w_planes[:, g, :, 127:255].rearrange("p t j -> p j t").unsqueeze(2).to_broadcast([P, 128, 2, 4]),
-            )
-            nc.vector.tensor_copy(
-                out=wg[:, g, 256:512, :],
-                in_=w_planes[:, g, :, 255:511].rearrange("p t j -> p j t"),
-            )
+            nc.vector.tensor_copy(out=wg_upper[:, g], in_=w_planes[:, g, :, 127:511].rearrange("p t j -> p j t"))
 
         def regroup_level_9(copy, g):
             copy(
-                out=wg[:, g, 512:1024, :].rearrange("p (c j) t -> p c j t", c=2),
+                out=wg_last[:, g].rearrange("p (c j) t -> p c j t", c=2),
                 in_=w_planes[:, g, :, 511:1023].rearrange("p t (j c) -> p c j t", c=2),
             )
 
-        def quantise_w(g, first):
+        def quantise_w(first, width):
             nc.vector.quantize_mx(
-                out=wc[:, g, first : first + 512].bitcast(FP8X4),
-                scales=ws[:, g, first : first + 512],
-                in_=wg[:, g, first : first + 512, :].rearrange("p n t -> p (n t)"),
+                out=wc[:, first : first + width].bitcast(FP8X4),
+                scales=ws[:, first : first + width],
+                in_=w_halves[:, first : first + width, :].rearrange("p n t -> p (n t)"),
             )
+
+        def w_first(slot, g):
+            if slot < 3:
+                return UPPER * g + P * slot
+            return PASSES * UPPER + LAST * g + P * (slot - 3)
 
         xg_of = {}
         xq_of = {}
@@ -181,7 +180,6 @@ def tile_treemodel_kernel(tc, x, W_gate, b_gate, leaf_logits_words, leaf_logits_
             )
 
         turn_of = {}
-        reach7_of = {}
 
         top_of = {}
 
@@ -204,46 +202,30 @@ def tile_treemodel_kernel(tc, x, W_gate, b_gate, leaf_logits_words, leaf_logits_
         def top_turns(n):
             if not live(n):
                 return
-            low = work.tile([P, 2, ROW_TILES, 64], F32, name="turn_low")
-            six = work.tile([P, 2, ROW_TILES, 64], F32, name="turn_six")
+            turn = work.tile([P, 2, ROW_TILES, TOP], F32, name="turn")
             for c, scale in ((1, 1.0), (0, -1.0)):
-                nc.scalar.activation(out=low[:, c, :, 0:63], in_=top_of[n][:, :, 0:63], func=SIGMOID, scale=scale)
-            for c, scale in ((1, 1.0), (0, -1.0)):
-                nc.scalar.activation(out=six[:, c], in_=top_of[n][:, :, 63:127], func=SIGMOID, scale=scale)
-            turn_of[n] = (low, six)
+                nc.scalar.activation(out=turn[:, c], in_=top_of[n][:], func=SIGMOID, scale=scale)
+            turn_of[n] = turn
 
         reach_of = {}
 
         def sweep_level(n, level):
             if not live(n):
                 return
-            low = turn_of[n][0]
+            turn = turn_of[n]
             nodes = 2**level
             if level == 1:
-                reach = low[:, :, :, 0].rearrange("p c q -> p q c")
+                reach = turn[:, :, :, 0].rearrange("p c q -> p q c")
             else:
                 reach = reach_of[n][:]
             children = work.tile([P, ROW_TILES, 2 * nodes], F32, name="reach%d" % (level + 1))
             nc.vector.tensor_tensor(
                 out=children[:].rearrange("p q (j c) -> p q j c", c=2),
                 in0=reach.unsqueeze(3).to_broadcast([P, ROW_TILES, nodes, 2]),
-                in1=low[:, :, :, nodes - 1 : 2 * nodes - 1].rearrange("p c q j -> p q j c"),
+                in1=turn[:, :, :, nodes - 1 : 2 * nodes - 1].rearrange("p c q j -> p q j c"),
                 op=ALU.mult,
             )
             reach_of[n] = children
-
-        def sweep_last(n):
-            if not live(n):
-                return
-            reach7 = work.tile([P, ROW_TILES, 256], F32, name="reach7")
-            shape = [P, ROW_TILES * 64, 2, 2]
-            nc.vector.tensor_tensor(
-                out=reach7[:].rearrange("p q (j c d) -> p (q j) c d", c=2, d=2),
-                in0=reach_of[n][:].rearrange("p q j -> p (q j)").unsqueeze(2).unsqueeze(3).to_broadcast(shape),
-                in1=turn_of[n][1][:].rearrange("p c q j -> p (q j) c").unsqueeze(3).to_broadcast(shape),
-                op=ALU.mult,
-            )
-            reach7_of[n] = reach7
 
         low_of = {}
         pt_of = {}
@@ -253,8 +235,8 @@ def tile_treemodel_kernel(tc, x, W_gate, b_gate, leaf_logits_words, leaf_logits_
             for g in range(PASSES):
                 nc.tensor.matmul_mx(
                     out=z[:],
-                    lhsT=wc[:, g, P * slot : P * slot + P].bitcast(FP8X4),
-                    lhsT_scale=ws[:, g, P * slot : P * slot + P],
+                    lhsT=wc[:, w_first(slot, g) : w_first(slot, g) + P].bitcast(FP8X4),
+                    lhsT_scale=ws[:, w_first(slot, g) : w_first(slot, g) + P],
                     rhs=xc[:, g, :].bitcast(FP8X4),
                     rhs_scale=xs[:, g, :],
                     start=(g == 0),
@@ -275,80 +257,90 @@ def tile_treemodel_kernel(tc, x, W_gate, b_gate, leaf_logits_words, leaf_logits_
             turn7, right8, turn9 = low_of[n]
             z = low_logits(xq_of[n][0], xq_of[n][1], slot)
             z_pieces = z[:].rearrange("p (h b) -> p h b", h=pieces)
-            if slot < 2:
+            if slot == 0:
+                nc.scalar.activation(out=turn7[:, 1, :], in_=z[:], func=SIGMOID, bias=column(64))
                 nc.scalar.activation(
-                    out=turn7[:, slot, :], in_=z[:], func=SIGMOID, bias=column(64 + slot), scale=column(96)
+                    out=turn7[:, 0, :], in_=z[:], func=SIGMOID, scale=-1.0, bias=bias_minus[:, 64:65]
                 )
-            elif slot < 4:
+            elif slot < 3:
                 nc.scalar.activation(
-                    out=right8[:, :, slot - 2, :], in_=z_pieces, func=SIGMOID, bias=column(32 + slot - 2)
+                    out=right8[:, :, slot - 1, :], in_=z_pieces, func=SIGMOID, bias=column(32 + slot - 1)
                 )
             else:
-                c, g9 = divmod(slot - 4, 2)
-                nc.scalar.activation(
-                    out=turn9[:, :, c, 1, g9, :], in_=z_pieces, func=SIGMOID, bias=column(slot - 4)
-                )
+                i = slot - 3
+                c, g9 = divmod(i, 2)
+                nc.scalar.activation(out=turn9[:, :, c, 1, g9, :], in_=z_pieces, func=SIGMOID, bias=column(i))
                 if c == 1:
                     nc.scalar.activation(
                         out=turn9[:, :, c, 0, g9, :], in_=z_pieces, func=SIGMOID, scale=-1.0,
-                        bias=bias_minus[:, slot - 4 : slot - 3],
+                        bias=bias_minus[:, i : i + 1],
                     )
 
-        def reach7_transpose(n):
+        def turn7_transpose(n):
             if not live(n):
                 return
-            reach7 = reach7_of[n]
+            turn7 = low_of[n][0]
             banks = []
-            for g in range(2):
-                pt = psum_pt.tile([P, CHUNK], F32)
-                for q in range(ROW_TILES):
-                    nc.tensor.transpose(
-                        out=pt[:, P * q : P * q + P],
-                        in_=reach7[:, q, P * g : P * g + P],
-                        identity=ident[:],
-                    )
+            for k in range(2):
+                pt = psum_pt.tile([P, 2, 2, P], F32, name="pt")
+                for c in range(2):
+                    for qq in range(2):
+                        first = P * (2 * k + qq)
+                        nc.tensor.transpose(
+                            out=pt[:, c, qq, :], in_=turn7[:, c, first : first + P], identity=ident[:]
+                        )
                 banks.append(pt)
-            pt_of[n] = banks
+            turn7_of[n] = banks
 
+        turn7_of = {}
         reach8_of = {}
         reach9_of = {}
         probs_of = {}
         pq_of = {}
 
-        def reach8(n, g):
+        def sweep_level_7(n, k):
             if not live(n):
                 return
-            pieces = pieces_of(n)
-            if g == 0:
-                reach8_of[n] = work.tile([P, pieces, 2, CHUNK // pieces], F32, name="reach8")
+            if k == 0:
+                reach8_of[n] = work.tile([P, ROW_TILES, 256], F32, name="reach8")
+            parent = reach_of[n][:, 2 * k : 2 * k + 2, :].rearrange("p q j -> p (q j)")
             nc.vector.tensor_tensor(
-                out=reach8_of[n][:, :, g, :],
-                in0=pt_of[n][g][:].rearrange("p (h b) -> p h b", h=pieces),
-                in1=low_of[n][0][:, g, :].rearrange("p (h b) -> p h b", h=pieces),
+                out=reach8_of[n][:, 2 * k : 2 * k + 2, :].rearrange("p q (j c) -> p (q j) c", c=2),
+                in0=parent.unsqueeze(2).to_broadcast([P, 256, 2]),
+                in1=turn7_of[n][k][:].rearrange("p c q j -> p (q j) c"),
                 op=ALU.mult,
             )
 
-        def by_four(ap):
-            return ap.rearrange("p h g b -> p (h g b)").rearrange("p (k i) -> p k i", i=4)
+        def reach8_transpose(n):
+            if not live(n):
+                return
+            banks = []
+            for g in range(2):
+                pt = psum_pt.tile([P, CHUNK], F32, name="pt")
+                for q in range(ROW_TILES):
+                    nc.tensor.transpose(
+                        out=pt[:, P * q : P * q + P],
+                        in_=reach8_of[n][:, q, P * g : P * g + P],
+                        identity=ident[:],
+                    )
+                banks.append(pt)
+            pt_of[n] = banks
 
-        def child9(n, c):
-            return reach9_of[n][:].rearrange("p h g k c i -> p (h g k) c i")[:, :, c, :]
-
-        def reach9(n, c):
+        def reach9(n, c, g):
             if not live(n):
                 return
             pieces = pieces_of(n)
-            if c == 1:
+            if c == 1 and g == 0:
                 reach9_of[n] = work.tile(
                     [P, pieces, 2, CHUNK // pieces // 4, 2, 4], F32, align_bytes=64, name="reach9"
                 )
-                nc.vector.tensor_tensor(
-                    out=child9(n, 1), in0=by_four(reach8_of[n][:]), in1=by_four(low_of[n][1][:]), op=ALU.mult
-                )
+            parent = pt_of[n][g][:].rearrange("p (h k i) -> p h k i", h=pieces, i=4)
+            right = reach9_of[n][:, :, g, :, 1, :]
+            if c == 1:
+                turn = low_of[n][1][:, :, g, :].rearrange("p h (k i) -> p h k i", i=4)
+                nc.vector.tensor_tensor(out=right, in0=parent, in1=turn, op=ALU.mult)
             else:
-                nc.vector.tensor_tensor(
-                    out=child9(n, 0), in0=by_four(reach8_of[n][:]), in1=child9(n, 1), op=ALU.subtract
-                )
+                nc.vector.tensor_tensor(out=reach9_of[n][:, :, g, :, 0, :], in0=parent, in1=right, op=ALU.subtract)
 
         def turn9_left(n):
             if not live(n):
@@ -420,67 +412,68 @@ def tile_treemodel_kernel(tc, x, W_gate, b_gate, leaf_logits_words, leaf_logits_
             elif half == 1:
                 nc.sync.dma_start(out=out_tiles[n, q], in_=rows_of[n][:])
 
-        def vector_period(n):
-            turn9_left(n)
-            sweep_level(n + 2, 1)
-            leaf_probs(n, 0)
-            sweep_level(n + 2, 2)
-            reach8(n + 1, 0)
-            sweep_level(n + 2, 3)
-            reach8(n + 1, 1)
-            leaf_quantise(n, 0)
-            sweep_level(n + 2, 4)
-            reach9(n + 1, 1)
-            leaf_probs(n, 1)
-            sweep_level(n + 2, 5)
-            reach9(n + 1, 0)
-            if pieces_of(n) == 4:
-                leaf_probs(n, 2)
-            leaf_quantise(n, 1)
-            if pieces_of(n) == 4:
-                leaf_probs(n, 3)
-                leaf_quantise(n, 2)
-                leaf_quantise(n, 3)
-            x_quantise(n + 3)
-            sweep_last(n + 2)
-
-        def front(n):
+        def top(n):
             for q in range(ROW_TILES):
                 top_logits(n, q)
             top_turns(n)
+
+        def x_in(n):
             for q in range(ROW_TILES):
-                x_transpose(n + 1, q // 2, q % 2)
+                x_transpose(n, q // 2, q % 2)
 
-        def late(n):
-            for i in range(4):
-                leaves(n - 1, 2 + i // 2, i % 2)
-                low_turn(n + 1, 4 + i)
+        def period(k):
+            for half in range(2):
+                low_turn(k - 2, half)
+                leaves(k - 4, 0, half)
+            top(k)
+            low_turn(k - 2, 2)
+            turn7_transpose(k - 2)
+            sweep_level(k - 1, 6)
+            leaf_probs(k - 3, 0)
+            x_quantise(k)
+            for half in range(2):
+                low_turn(k - 2, 3 + half)
+                leaves(k - 4, 1, half)
+            sweep_level_7(k - 2, 0)
+            sweep_level(k, 1)
+            leaf_quantise(k - 3, 0)
+            sweep_level(k, 2)
+            sweep_level_7(k - 2, 1)
+            sweep_level(k, 3)
+            for half in range(2):
+                low_turn(k - 2, 5 + half)
+                leaves(k - 4, 2, half)
+            turn9_left(k - 2)
+            reach8_transpose(k - 2)
+            leaf_probs(k - 3, 1)
+            sweep_level(k, 4)
+            if k - 3 == CHUNKS - 1:
+                leaf_quantise(k - 3, 1)
+                leaf_probs(k - 3, 2)
+                leaf_quantise(k - 3, 2)
+                leaf_probs(k - 3, 3)
+                leaf_quantise(k - 3, 3)
+            reach9(k - 2, 1, 0)
+            sweep_level(k, 5)
+            reach9(k - 2, 1, 1)
+            if k - 3 != CHUNKS - 1:
+                leaf_quantise(k - 3, 1)
+            reach9(k - 2, 0, 0)
+            reach9(k - 2, 0, 1)
+            for half in range(2):
+                leaves(k - 4, 3, half)
+            x_in(k + 1)
 
-        def early(n):
-            for i in range(4):
-                leaves(n, i // 2, i % 2)
-                low_turn(n + 2, i)
-            reach7_transpose(n + 2)
-
-        def tensor_period(n):
-            late(n)
-            front(n + 3)
-            early(n)
-
-        tensor_period(-4)
+        x_in(0)
         spread_bias()
-        vector_period(-3)
-        tensor_period(-3)
         regroup_levels_7_8(0)
         regroup_level_9(nc.vector.tensor_copy, 0)
+        period(0)
         regroup_level_9(nc.scalar.copy, 1)
         regroup_levels_7_8(1)
-        for g in range(PASSES):
-            quantise_w(g, 0)
-        vector_period(-2)
-        for g in range(PASSES):
-            quantise_w(g, 512)
-        for n in range(-2, CHUNKS + 1):
-            if n > -2:
-                vector_period(n)
-            tensor_period(n)
+        quantise_w(0, 512)
+        quantise_w(512, 256)
+        period(1)
+        quantise_w(PASSES * UPPER, PASSES * LAST)
+        for k in range(2, CHUNKS + 4):
+            period(k)

@@ -36,7 +36,7 @@ def tile_treemodel_kernel(tc, x, W_gate, b_gate, leaf_logits_words, leaf_logits_
         work = ctx.enter_context(tc.tile_pool(name="work", bufs=2))
         xqp = ctx.enter_context(tc.tile_pool(name="xqp", bufs=3))
         turns = ctx.enter_context(tc.tile_pool(name="turns", bufs=2))
-        ostage = ctx.enter_context(tc.tile_pool(name="ostage", bufs=4))
+        ostage = ctx.enter_context(tc.tile_pool(name="ostage", bufs=8))
         psum_stream = ctx.enter_context(tc.psum_pool(name="psum_stream", bufs=5))
         psum_top = ctx.enter_context(tc.psum_pool(name="psum_top", bufs=1))
         psum_pt = ctx.enter_context(tc.psum_pool(name="psum_pt", bufs=2))
@@ -70,9 +70,9 @@ def tile_treemodel_kernel(tc, x, W_gate, b_gate, leaf_logits_words, leaf_logits_
         w_top = const.tile([P, 4, 2, TOP], BF16)
         top_rows = W_gate.rearrange("(a p e) c -> e p a c", a=4, p=P, e=2)
         nc.sync.dma_start(out=x_rows[0][:, 0:2, :], in_=x_chunks[0][:, 0:2, :])
+        nc.sync.dma_start(out=x_rows[0][:, 2:4, :], in_=x_chunks[0][:, 2:4, :])
         for e in range(2):
             nc.sync.dma_start(out=w_top[:, :, e, :], in_=top_rows[e][:, :, 0:TOP])
-        nc.sync.dma_start(out=x_rows[0][:, 2:4, :], in_=x_chunks[0][:, 2:4, :])
         for a in range(2):
             nc.sync.dma_start(out=w_raw[:, a, :, 0:1023], in_=w_rows[a])
         nc.sync.dma_start(out=x_rows[1][:], in_=x_chunks[1])
@@ -421,59 +421,66 @@ def tile_treemodel_kernel(tc, x, W_gate, b_gate, leaf_logits_words, leaf_logits_
             for q in range(ROW_TILES):
                 x_transpose(n, q // 2, q % 2)
 
-        def period(k):
-            for half in range(2):
-                low_turn(k - 2, half)
-                leaves(k - 4, 0, half)
-            top(k)
-            low_turn(k - 2, 2)
-            turn7_transpose(k - 2)
-            sweep_level(k - 1, 6)
-            leaf_probs(k - 3, 0)
-            x_quantise(k)
-            for half in range(2):
-                low_turn(k - 2, 3 + half)
-                leaves(k - 4, 1, half)
-            sweep_level_7(k - 2, 0)
-            sweep_level(k, 1)
-            leaf_quantise(k - 3, 0)
-            sweep_level(k, 2)
-            sweep_level_7(k - 2, 1)
-            sweep_level(k, 3)
-            for half in range(2):
-                low_turn(k - 2, 5 + half)
-                leaves(k - 4, 2, half)
-            turn9_left(k - 2)
-            reach8_transpose(k - 2)
-            leaf_probs(k - 3, 1)
-            sweep_level(k, 4)
-            if k - 3 == CHUNKS - 1:
-                leaf_quantise(k - 3, 1)
-                leaf_probs(k - 3, 2)
-                leaf_quantise(k - 3, 2)
-                leaf_probs(k - 3, 3)
-                leaf_quantise(k - 3, 3)
-            reach9(k - 2, 1, 0)
-            sweep_level(k, 5)
-            reach9(k - 2, 1, 1)
-            if k - 3 != CHUNKS - 1:
-                leaf_quantise(k - 3, 1)
-            reach9(k - 2, 0, 0)
-            reach9(k - 2, 0, 1)
-            for half in range(2):
-                leaves(k - 4, 3, half)
-            x_in(k + 1)
+        def period(f):
+            sweep_level(f - 2, 5)
+            leaf_probs(f - 3, 0)
+            sweep_level(f - 2, 6)
+            leaves(f - 4, 2, 0)
+            low_turn(f - 2, 2)
+            low_turn(f - 2, 3)
+            if f - 3 == CHUNKS - 1:
+                leaf_probs(f - 3, 1)
+            leaf_quantise(f - 3, 0)
+            sweep_level(f - 1, 1)
+            leaves(f - 4, 2, 1)
+            low_turn(f - 2, 6)
+            sweep_level_7(f - 2, 0)
+            sweep_level(f - 1, 2)
+            sweep_level_7(f - 2, 1)
+            sweep_level(f - 1, 3)
+            leaves(f - 4, 3, 0)
+            reach8_transpose(f - 2)
+            leaves(f - 4, 3, 1)
+            if f - 3 == CHUNKS - 1:
+                leaf_probs(f - 3, 2)
+                leaf_quantise(f - 3, 1)
+                leaf_probs(f - 3, 3)
+                leaf_quantise(f - 3, 2)
+                leaf_quantise(f - 3, 3)
+            else:
+                leaf_probs(f - 3, 1)
+            sweep_level(f - 1, 4)
+            x_quantise(f)
+            low_turn(f - 2, 4)
+            low_turn(f - 2, 5)
+            leaves(f - 3, 0, 0)
+            reach9(f - 2, 1, 0)
+            reach9(f - 2, 1, 1)
+            low_turn(f - 1, 0)
+            low_turn(f - 1, 1)
+            leaves(f - 3, 0, 1)
+            leaves(f - 3, 1, 0)
+            leaves(f - 3, 1, 1)
+            reach9(f - 2, 0, 0)
+            turn9_left(f - 2)
+            reach9(f - 2, 0, 1)
+            if f - 3 != CHUNKS - 1:
+                leaf_quantise(f - 3, 1)
+            top(f)
+            turn7_transpose(f - 1)
 
         x_in(0)
         spread_bias()
         regroup_levels_7_8(0)
         regroup_level_9(nc.vector.tensor_copy, 0)
         period(0)
-        regroup_level_9(nc.scalar.copy, 1)
         regroup_levels_7_8(1)
         quantise_w(0, 512)
         quantise_w(512, 256)
+        x_in(1)
+        regroup_level_9(nc.scalar.copy, 1)
         period(1)
         quantise_w(PASSES * UPPER, PASSES * LAST)
-        for k in range(2, CHUNKS + 4):
-            period(k)
+        for f in range(2, CHUNKS + 4):
+            x_in(f)
+            period(f)

@@ -75,9 +75,9 @@ def tile_treemodel_kernel(tc, x, W_gate, b_gate, leaf_logits_words, leaf_logits_
             nc.sync.dma_start(out=w_top[:, :, e, :], in_=top_rows[e][:, :, 0:TOP])
         for a in range(2):
             nc.sync.dma_start(out=w_raw[:, a, :, 0:1023], in_=w_rows[a])
-        nc.sync.dma_start(out=x_rows[1][:], in_=x_chunks[1])
         for a in range(2, 4):
             nc.sync.dma_start(out=w_raw[:, a, :, 0:1023], in_=w_rows[a])
+        nc.sync.dma_start(out=x_rows[1][:], in_=x_chunks[1])
         w_planes = w_raw[:].rearrange("p (g u) e c -> p g (u e) c", g=PASSES)
         top_planes = w_top[:].rearrange("p (g u) e c -> p g (u e) c", g=PASSES)
         for n in range(2, CHUNKS):
@@ -99,6 +99,8 @@ def tile_treemodel_kernel(tc, x, W_gate, b_gate, leaf_logits_words, leaf_logits_
         make_identity(nc, ident[:])
         ones = const.tile([P, P], BF16)
         nc.vector.memset(ones[:], 1.0)
+        dummy = const.tile([P, 512], BF16)
+        nc.vector.memset(dummy[:], 0.0)
         warm_in = const.tile([P, 1], F32)
         warm_out = const.tile([P, 1], F32)
         nc.vector.memset(warm_in[:], 0.0)
@@ -116,6 +118,11 @@ def tile_treemodel_kernel(tc, x, W_gate, b_gate, leaf_logits_words, leaf_logits_
             nc.tensor.transpose(out=b_ps[:], in_=b_all[:], identity=ident[:])
             nc.vector.tensor_copy(out=bias_cols[:], in_=b_ps[:])
             nc.vector.tensor_scalar_mul(out=bias_minus[:], in0=bias_cols[:], scalar1=-1.0)
+
+        def warm_up(count):
+            scratch = psum_stream.tile([P, 512], F32, name="stream")
+            for i in range(count):
+                nc.tensor.matmul(out=scratch[:], lhsT=ones[:], rhs=dummy[:], start=True, stop=True)
 
         def column(i):
             return bias_cols[:, i : i + 1]
@@ -422,65 +429,67 @@ def tile_treemodel_kernel(tc, x, W_gate, b_gate, leaf_logits_words, leaf_logits_
                 x_transpose(n, q // 2, q % 2)
 
         def period(f):
-            sweep_level(f - 2, 5)
-            leaf_probs(f - 3, 0)
-            sweep_level(f - 2, 6)
-            leaves(f - 4, 2, 0)
-            low_turn(f - 2, 2)
-            low_turn(f - 2, 3)
-            if f - 3 == CHUNKS - 1:
-                leaf_probs(f - 3, 1)
-            leaf_quantise(f - 3, 0)
-            sweep_level(f - 1, 1)
-            leaves(f - 4, 2, 1)
-            low_turn(f - 2, 6)
-            sweep_level_7(f - 2, 0)
-            sweep_level(f - 1, 2)
-            sweep_level_7(f - 2, 1)
-            sweep_level(f - 1, 3)
-            leaves(f - 4, 3, 0)
-            reach8_transpose(f - 2)
-            leaves(f - 4, 3, 1)
-            if f - 3 == CHUNKS - 1:
-                leaf_probs(f - 3, 2)
-                leaf_quantise(f - 3, 1)
-                leaf_probs(f - 3, 3)
-                leaf_quantise(f - 3, 2)
-                leaf_quantise(f - 3, 3)
-            else:
-                leaf_probs(f - 3, 1)
-            sweep_level(f - 1, 4)
-            x_quantise(f)
-            low_turn(f - 2, 4)
-            low_turn(f - 2, 5)
-            leaves(f - 3, 0, 0)
-            reach9(f - 2, 1, 0)
-            reach9(f - 2, 1, 1)
             low_turn(f - 1, 0)
-            low_turn(f - 1, 1)
-            leaves(f - 3, 0, 1)
-            leaves(f - 3, 1, 0)
-            leaves(f - 3, 1, 1)
+            x_in(f)
+            sweep_level(f - 1, 4)
             reach9(f - 2, 0, 0)
-            turn9_left(f - 2)
             reach9(f - 2, 0, 1)
+            turn9_left(f - 2)
             if f - 3 != CHUNKS - 1:
                 leaf_quantise(f - 3, 1)
+            leaves(f - 3, 0, 0)
+            low_turn(f - 1, 5)
+            leaves(f - 3, 0, 1)
+            leaves(f - 3, 1, 0)
+            sweep_level(f - 1, 5)
+            leaf_probs(f - 2, 0)
+            if f - 2 == CHUNKS - 1:
+                leaf_probs(f - 2, 1)
+            sweep_level(f - 1, 6)
+            leaf_quantise(f - 2, 0)
+            x_quantise(f)
             top(f)
             turn7_transpose(f - 1)
+            leaves(f - 3, 1, 1)
+            low_turn(f - 1, 1)
+            sweep_level_7(f - 1, 0)
+            leaves(f - 3, 2, 0)
+            low_turn(f - 1, 2)
+            sweep_level(f, 1)
+            sweep_level_7(f - 1, 1)
+            low_turn(f - 1, 6)
+            sweep_level(f, 2)
+            reach8_transpose(f - 1)
+            leaves(f - 3, 2, 1)
+            if f - 2 == CHUNKS - 1:
+                leaf_probs(f - 2, 2)
+                leaf_quantise(f - 2, 1)
+                leaf_probs(f - 2, 3)
+                leaf_quantise(f - 2, 2)
+                leaf_quantise(f - 2, 3)
+            else:
+                leaf_probs(f - 2, 1)
+            low_turn(f - 1, 3)
+            low_turn(f - 1, 4)
+            sweep_level(f, 3)
+            reach9(f - 1, 1, 0)
+            reach9(f - 1, 1, 1)
+            for half in range(2):
+                leaves(f - 3, 3, half)
 
+        warm_up(4)
         x_in(0)
         spread_bias()
+        x_quantise(0)
+        top(0)
         regroup_levels_7_8(0)
-        regroup_level_9(nc.vector.tensor_copy, 0)
-        period(0)
         regroup_levels_7_8(1)
-        quantise_w(0, 512)
-        quantise_w(512, 256)
-        x_in(1)
         regroup_level_9(nc.scalar.copy, 1)
-        period(1)
+        quantise_w(0, 512)
+        regroup_level_9(nc.vector.tensor_copy, 0)
         quantise_w(PASSES * UPPER, PASSES * LAST)
-        for f in range(2, CHUNKS + 4):
-            x_in(f)
+        quantise_w(512, 256)
+        for level in range(1, 4):
+            sweep_level(0, level)
+        for f in range(1, CHUNKS + 3):
             period(f)

@@ -134,13 +134,16 @@ def tile_treemodel_kernel(tc, x, W_gate, b_gate, leaf_logits_words, leaf_logits_
         ws = const.tile([P, PASSES * (UPPER + LAST)], U8, align_bytes=64)
 
         def regroup_levels_7_8(g):
-            nc.vector.tensor_copy(out=wg_upper[:, g], in_=w_planes[:, g, :, 127:511].rearrange("p t j -> p j t"))
+            nc.vector.tensor_copy(
+                out=wg_upper[:, g].rearrange("p (c i) t -> p c t i", i=4),
+                in_=w_planes[:, g, :, 127:511].rearrange("p t (c i) -> p c t i", i=4),
+            )
 
         def regroup_level_9(copy, g):
-            copy(
-                out=wg_last[:, g].rearrange("p (c j) t -> p c j t", c=2),
-                in_=w_planes[:, g, :, 511:1023].rearrange("p t (j c) -> p c j t", c=2),
-            )
+            sides_out = wg_last[:, g].rearrange("p (c j i) t -> p c j t i", c=2, i=4)
+            sides_in = w_planes[:, g, :, 511:1023].rearrange("p t (j i c) -> p c j t i", c=2, i=4)
+            for c in range(2):
+                copy(out=sides_out[:, c], in_=sides_in[:, c])
 
         def quantise_w(first, width):
             nc.vector.quantize_mx(
@@ -464,8 +467,8 @@ def tile_treemodel_kernel(tc, x, W_gate, b_gate, leaf_logits_words, leaf_logits_
             if f - 2 == CHUNKS - 1:
                 leaf_probs(f - 2, 2)
                 leaf_quantise(f - 2, 1)
-                leaf_probs(f - 2, 3)
                 leaf_quantise(f - 2, 2)
+                leaf_probs(f - 2, 3)
                 leaf_quantise(f - 2, 3)
             else:
                 leaf_probs(f - 2, 1)

@@ -11,6 +11,7 @@ U8 = mybir.dt.uint8
 FP8X4 = mybir.dt.float8_e4m3fn_x4
 ALU = mybir.AluOpType
 SIGMOID = mybir.ActivationFunctionType.Sigmoid
+IDENTITY = mybir.ActivationFunctionType.Identity
 
 P = 128
 BATCH = 2048
@@ -36,7 +37,7 @@ def tile_treemodel_kernel(tc, x, W_gate, b_gate, leaf_logits_words, leaf_logits_
         work = ctx.enter_context(tc.tile_pool(name="work", bufs=2))
         xqp = ctx.enter_context(tc.tile_pool(name="xqp", bufs=3))
         turns = ctx.enter_context(tc.tile_pool(name="turns", bufs=2))
-        ostage = ctx.enter_context(tc.tile_pool(name="ostage", bufs=8))
+        ostage = ctx.enter_context(tc.tile_pool(name="ostage", bufs=7))
         psum_stream = ctx.enter_context(tc.psum_pool(name="psum_stream", bufs=5))
         psum_top = ctx.enter_context(tc.psum_pool(name="psum_top", bufs=1))
         psum_pt = ctx.enter_context(tc.psum_pool(name="psum_pt", bufs=2))
@@ -51,6 +52,14 @@ def tile_treemodel_kernel(tc, x, W_gate, b_gate, leaf_logits_words, leaf_logits_
         def pieces_of(n):
             return 4 if n == CHUNKS - 1 else 2
 
+        warm_in = const.tile([P, 1], F32)
+        warm_out = const.tile([P, 1], F32)
+        nc.vector.memset(warm_in[:], 0.0)
+        nc.scalar.activation(out=warm_out[:], in_=warm_in[:], func=SIGMOID)
+        ones = const.tile([P, P], BF16)
+        nc.vector.memset(ones[:], 1.0)
+        dummy = const.tile([P, 512], BF16)
+        nc.vector.memset(dummy[:], 0.0)
         bias_row = const.tile([P, TOP], BF16)
         nc.vector.memset(bias_row[:], 0.0)
         b_src = const.tile([P, 256], BF16)
@@ -97,14 +106,6 @@ def tile_treemodel_kernel(tc, x, W_gate, b_gate, leaf_logits_words, leaf_logits_
 
         ident = const.tile([P, P], F32)
         make_identity(nc, ident[:])
-        ones = const.tile([P, P], BF16)
-        nc.vector.memset(ones[:], 1.0)
-        dummy = const.tile([P, 512], BF16)
-        nc.vector.memset(dummy[:], 0.0)
-        warm_in = const.tile([P, 1], F32)
-        warm_out = const.tile([P, 1], F32)
-        nc.vector.memset(warm_in[:], 0.0)
-        nc.scalar.activation(out=warm_out[:], in_=warm_in[:], func=SIGMOID)
 
         b_all = const.tile([P, P], F32)
         nc.vector.tensor_copy(out=b_all[0:32, :], in_=b_src[0:32, 0:256:2])
@@ -254,24 +255,24 @@ def tile_treemodel_kernel(tc, x, W_gate, b_gate, leaf_logits_words, leaf_logits_
                 )
             return z
 
+        logits7_of = {}
+
         def low_turn(n, slot):
             if not live(n):
                 return
             pieces = pieces_of(n)
             width = CHUNK // pieces
             if slot == 0:
-                turn7 = work.tile([P, 2, CHUNK], F32)
+                logits7_of[n] = work.tile([P, CHUNK], F32, name="logits7")
+            elif n not in low_of:
                 right8 = work.tile([P, pieces, 2, width], F32)
                 turn9 = turns.tile([P, pieces, 2, 2, 2, width], F32, align_bytes=64, name="turn9")
-                low_of[n] = (turn7, right8, turn9)
-            turn7, right8, turn9 = low_of[n]
+                low_of[n] = (None, right8, turn9)
+            right8, turn9 = low_of[n][1:] if slot > 0 else (None, None)
             z = low_logits(xq_of[n][0], xq_of[n][1], slot)
             z_pieces = z[:].rearrange("p (h b) -> p h b", h=pieces)
             if slot == 0:
-                nc.scalar.activation(out=turn7[:, 1, :], in_=z[:], func=SIGMOID, bias=column(64))
-                nc.scalar.activation(
-                    out=turn7[:, 0, :], in_=z[:], func=SIGMOID, scale=-1.0, bias=bias_minus[:, 64:65]
-                )
+                nc.scalar.activation(out=logits7_of[n][:], in_=z[:], func=IDENTITY, bias=column(64))
             elif slot < 3:
                 nc.scalar.activation(
                     out=right8[:, :, slot - 1, :], in_=z_pieces, func=SIGMOID, bias=column(32 + slot - 1)
@@ -280,27 +281,19 @@ def tile_treemodel_kernel(tc, x, W_gate, b_gate, leaf_logits_words, leaf_logits_
                 i = slot - 3
                 c, g9 = divmod(i, 2)
                 nc.scalar.activation(out=turn9[:, :, c, 1, g9, :], in_=z_pieces, func=SIGMOID, bias=column(i))
-                if c == 1:
-                    nc.scalar.activation(
-                        out=turn9[:, :, c, 0, g9, :], in_=z_pieces, func=SIGMOID, scale=-1.0,
-                        bias=bias_minus[:, i : i + 1],
-                    )
 
         def turn7_transpose(n):
             if not live(n):
                 return
-            turn7 = low_of[n][0]
-            banks = []
-            for k in range(2):
-                pt = psum_pt.tile([P, 2, 2, P], F32, name="pt")
-                for c in range(2):
-                    for qq in range(2):
-                        first = P * (2 * k + qq)
-                        nc.tensor.transpose(
-                            out=pt[:, c, qq, :], in_=turn7[:, c, first : first + P], identity=ident[:]
-                        )
-                banks.append(pt)
-            turn7_of[n] = banks
+            pt = psum_stream.tile([P, ROW_TILES, P], F32, name="stream")
+            for q in range(ROW_TILES):
+                nc.tensor.transpose(
+                    out=pt[:, q, :], in_=logits7_of[n][:, P * q : P * q + P], identity=ident[:]
+                )
+            turn7 = work.tile([P, 2, ROW_TILES, P], F32, name="turn7")
+            for c, scale in ((1, 1.0), (0, -1.0)):
+                nc.scalar.activation(out=turn7[:, c], in_=pt[:], func=SIGMOID, scale=scale)
+            turn7_of[n] = turn7
 
         turn7_of = {}
         reach8_of = {}
@@ -308,16 +301,14 @@ def tile_treemodel_kernel(tc, x, W_gate, b_gate, leaf_logits_words, leaf_logits_
         probs_of = {}
         pq_of = {}
 
-        def sweep_level_7(n, k):
+        def sweep_level_7(n):
             if not live(n):
                 return
-            if k == 0:
-                reach8_of[n] = work.tile([P, ROW_TILES, 256], F32, name="reach8")
-            parent = reach_of[n][:, 2 * k : 2 * k + 2, :].rearrange("p q j -> p (q j)")
+            reach8_of[n] = work.tile([P, ROW_TILES, 256], F32, name="reach8")
             nc.vector.tensor_tensor(
-                out=reach8_of[n][:, 2 * k : 2 * k + 2, :].rearrange("p q (j c) -> p (q j) c", c=2),
-                in0=parent.unsqueeze(2).to_broadcast([P, 256, 2]),
-                in1=turn7_of[n][k][:].rearrange("p c q j -> p (q j) c"),
+                out=reach8_of[n][:].rearrange("p q (j c) -> p (q j) c", c=2),
+                in0=reach_of[n][:].rearrange("p q j -> p (q j)").unsqueeze(2).to_broadcast([P, ROW_TILES * P, 2]),
+                in1=turn7_of[n][:].rearrange("p c q j -> p (q j) c"),
                 op=ALU.mult,
             )
 
@@ -355,10 +346,25 @@ def tile_treemodel_kernel(tc, x, W_gate, b_gate, leaf_logits_words, leaf_logits_
         def turn9_left(n):
             if not live(n):
                 return
+            minus = work.tile([P, 1], F32, name="minus")
+            nc.vector.memset(minus[:], -1.0)
+            turn9 = low_of[n][2]
+            nc.gpsimd.tensor_scalar(
+                out=turn9[:, :, 1, 0].rearrange("p h g b -> p h (g b)"),
+                in0=turn9[:, :, 1, 1].rearrange("p h g b -> p h (g b)"),
+                scalar1=minus[:], scalar2=1.0, op0=ALU.mult, op1=ALU.add,
+            )
+            nc.gpsimd.tensor_scalar(
+                out=turn9[:, :, 0, 0, 0], in0=turn9[:, :, 0, 1, 0],
+                scalar1=minus[:], scalar2=1.0, op0=ALU.mult, op1=ALU.add,
+            )
+
+        def turn9_v(n):
+            if not live(n):
+                return
             turn9 = low_of[n][2]
             nc.vector.tensor_scalar(
-                out=turn9[:, :, 0, 0].rearrange("p h g b -> p h (g b)"),
-                in0=turn9[:, :, 0, 1].rearrange("p h g b -> p h (g b)"),
+                out=turn9[:, :, 0, 0, 1], in0=turn9[:, :, 0, 1, 1],
                 scalar1=-1.0, scalar2=1.0, op0=ALU.mult, op1=ALU.add,
             )
 
@@ -432,12 +438,12 @@ def tile_treemodel_kernel(tc, x, W_gate, b_gate, leaf_logits_words, leaf_logits_
                 x_transpose(n, q // 2, q % 2)
 
         def period(f):
-            low_turn(f - 1, 0)
             x_in(f)
-            sweep_level(f - 1, 4)
+            turn7_transpose(f - 1)
             reach9(f - 2, 0, 0)
             reach9(f - 2, 0, 1)
-            turn9_left(f - 2)
+            turn9_v(f - 2)
+            sweep_level(f - 1, 4)
             if f - 3 != CHUNKS - 1:
                 leaf_quantise(f - 3, 1)
             leaves(f - 3, 0, 0)
@@ -450,16 +456,14 @@ def tile_treemodel_kernel(tc, x, W_gate, b_gate, leaf_logits_words, leaf_logits_
                 leaf_probs(f - 2, 1)
             sweep_level(f - 1, 6)
             leaf_quantise(f - 2, 0)
+            sweep_level_7(f - 1)
             x_quantise(f)
             top(f)
-            turn7_transpose(f - 1)
             leaves(f - 3, 1, 1)
             low_turn(f - 1, 1)
-            sweep_level_7(f - 1, 0)
             leaves(f - 3, 2, 0)
             low_turn(f - 1, 2)
             sweep_level(f, 1)
-            sweep_level_7(f - 1, 1)
             low_turn(f - 1, 6)
             sweep_level(f, 2)
             reach8_transpose(f - 1)
@@ -475,16 +479,19 @@ def tile_treemodel_kernel(tc, x, W_gate, b_gate, leaf_logits_words, leaf_logits_
             low_turn(f - 1, 3)
             low_turn(f - 1, 4)
             sweep_level(f, 3)
+            turn9_left(f - 1)
             reach9(f - 1, 1, 0)
             reach9(f - 1, 1, 1)
+            low_turn(f, 0)
             for half in range(2):
                 leaves(f - 3, 3, half)
 
-        warm_up(4)
+        warm_up(3)
         x_in(0)
         spread_bias()
         x_quantise(0)
         top(0)
+        warm_up(8)
         regroup_levels_7_8(0)
         regroup_levels_7_8(1)
         regroup_level_9(nc.scalar.copy, 1)
@@ -494,5 +501,6 @@ def tile_treemodel_kernel(tc, x, W_gate, b_gate, leaf_logits_words, leaf_logits_
         quantise_w(512, 256)
         for level in range(1, 4):
             sweep_level(0, level)
+        low_turn(0, 0)
         for f in range(1, CHUNKS + 3):
             period(f)

from contextlib import ExitStack

import concourse.mybir as mybir
from concourse.masks import make_identity

F32 = mybir.dt.float32
BF16 = mybir.dt.bfloat16
I32 = mybir.dt.int32
U32 = mybir.dt.uint32
U8 = mybir.dt.uint8
FP8X4 = mybir.dt.float8_e4m3fn_x4
ALU = mybir.AluOpType
SIGMOID = mybir.ActivationFunctionType.Sigmoid
IDENTITY = mybir.ActivationFunctionType.Identity

P = 128
BATCH = 2048
FEATURES = 1024
CLASSES = 1024
PASSES = 2
CHUNK = 512
HALF = CHUNK // 2
ROW_TILES = CHUNK // P
CHUNKS = BATCH // CHUNK
TOP = 128
UPPER = 384
LAST = 512

FLOPS = 2 * BATCH * FEATURES * (TOP + 896) + 2 * BATCH * 1024 * CLASSES


def tile_treemodel_kernel(tc, x, W_gate, b_gate, leaf_logits_words, leaf_logits_scales, out):
    nc = tc.nc
    with ExitStack() as ctx:
        const = ctx.enter_context(tc.tile_pool(name="const", bufs=1))
        xin = ctx.enter_context(tc.tile_pool(name="xin", bufs=CHUNKS))
        work = ctx.enter_context(tc.tile_pool(name="work", bufs=2))
        xqp = ctx.enter_context(tc.tile_pool(name="xqp", bufs=3))
        turns = ctx.enter_context(tc.tile_pool(name="turns", bufs=2))
        ostage = ctx.enter_context(tc.tile_pool(name="ostage", bufs=7))
        psum_stream = ctx.enter_context(tc.psum_pool(name="psum_stream", bufs=5))
        psum_top = ctx.enter_context(tc.psum_pool(name="psum_top", bufs=1))
        psum_pt = ctx.enter_context(tc.psum_pool(name="psum_pt", bufs=2))
        ctx.enter_context(tc.manual_schedule())

        x_chunks = x.rearrange("(n p q) k -> n p q k", p=P, q=ROW_TILES)
        out_tiles = out.rearrange("(n p q) c -> n q p c", p=P, q=ROW_TILES)

        def live(n):
            return 0 <= n < CHUNKS

        def pieces_of(n):
            return 4 if n == CHUNKS - 1 else 2

        warm_in = const.tile([P, 1], F32)
        warm_out = const.tile([P, 1], F32)
        nc.vector.memset(warm_in[:], 0.0)
        nc.scalar.activation(out=warm_out[:], in_=warm_in[:], func=SIGMOID)
        ones = const.tile([P, P], BF16)
        nc.vector.memset(ones[:], 1.0)
        dummy = const.tile([P, 512], BF16)
        nc.vector.memset(dummy[:], 0.0)
        bias_row = const.tile([P, TOP], BF16)
        nc.vector.memset(bias_row[:], 0.0)
        b_src = const.tile([P, 256], BF16)
        nc.vector.memset(b_src[:], 0.0)
        nc.scalar.dma_start(out=bias_row[0:1, :], in_=b_gate[0:TOP].rearrange("(o m) -> o m", o=1))
        level9_bias = b_gate[511:1023].rearrange("(g m) -> g m", g=2)
        for c in range(2):
            nc.scalar.dma_start(out=b_src[2 * c : 2 * c + 2, 0:255], in_=level9_bias[:, c : c + 255])
        nc.scalar.dma_start(out=b_src[32:34, 0:128], in_=b_gate[255:511].rearrange("(g m) -> g m", g=2))
        nc.scalar.dma_start(out=b_src[64:65, 0:128], in_=b_gate[127:255].rearrange("(o m) -> o m", o=1))

        x_rows = []
        for n in range(CHUNKS):
            x_rows.append(xin.tile([P, ROW_TILES, FEATURES], BF16, name="x_sb"))
        w_raw = turns.tile([P, 4, 2, 1024], BF16, align_bytes=64, name="turn9")
        w_rows = W_gate.rearrange("(a p e) c -> a p e c", a=4, p=P, e=2)
        w_top = const.tile([P, 4, 2, TOP], BF16)
        top_rows = W_gate.rearrange("(a p e) c -> e p a c", a=4, p=P, e=2)
        nc.sync.dma_start(out=x_rows[0][:, 0:2, :], in_=x_chunks[0][:, 0:2, :])
        nc.sync.dma_start(out=x_rows[0][:, 2:4, :], in_=x_chunks[0][:, 2:4, :])
        for e in range(2):
            nc.sync.dma_start(out=w_top[:, :, e, :], in_=top_rows[e][:, :, 0:TOP])
        for a in range(2):
            nc.sync.dma_start(out=w_raw[:, a, :, 0:1023], in_=w_rows[a])
        for a in range(2, 4):
            nc.sync.dma_start(out=w_raw[:, a, :, 0:1023], in_=w_rows[a])
        nc.sync.dma_start(out=x_rows[1][:], in_=x_chunks[1])
        w_planes = w_raw[:].rearrange("p (g u) e c -> p g (u e) c", g=PASSES)
        top_planes = w_top[:].rearrange("p (g u) e c -> p g (u e) c", g=PASSES)
        for n in range(2, CHUNKS):
            nc.sync.dma_start(out=x_rows[n][:], in_=x_chunks[n])

        leaf_scales = const.tile([P, PASSES, CLASSES], U8, align_bytes=64)
        nc.vector.memset(leaf_scales[:].rearrange("p g n -> p (g n)").bitcast(I32), 0)
        scale_rows = leaf_logits_scales.rearrange("g (k r) n -> r k g n", r=4)
        for r in range(4):
            nc.sync.dma_start(out=leaf_scales[r:P:32, :, :].bitcast(I32), in_=scale_rows[r].bitcast(I32))
        leaf_words = const.tile([P, PASSES, 4 * CLASSES], U8, align_bytes=64)
        for g in range(PASSES):
            nc.sync.dma_start(
                out=leaf_words[:, g, :].bitcast(I32),
                in_=leaf_logits_words[g].rearrange("p n t -> p (n t)").bitcast(I32),
            )

        ident = const.tile([P, P], F32)
        make_identity(nc, ident[:])

        b_all = const.tile([P, P], F32)
        nc.vector.tensor_copy(out=b_all[0:32, :], in_=b_src[0:32, 0:256:2])
        nc.vector.tensor_copy(out=b_all[32:64, :], in_=b_src[32:64, 0:128])
        nc.vector.tensor_copy(out=b_all[64:128, :], in_=b_src[64:128, 0:128])
        bias_cols = const.tile([P, P], F32)
        bias_minus = const.tile([P, P], F32)

        def spread_bias():
            b_ps = psum_pt.tile([P, P], F32, name="pt")
            nc.tensor.transpose(out=b_ps[:], in_=b_all[:], identity=ident[:])
            nc.vector.tensor_copy(out=bias_cols[:], in_=b_ps[:])
            nc.vector.tensor_scalar_mul(out=bias_minus[:], in0=bias_cols[:], scalar1=-1.0)

        def warm_up(count):
            scratch = psum_stream.tile([P, 512], F32, name="stream")
            for i in range(count):
                nc.tensor.matmul(out=scratch[:], lhsT=ones[:], rhs=dummy[:], start=True, stop=True)

        def column(i):
            return bias_cols[:, i : i + 1]

        w_halves = turns.tile([P, PASSES * (UPPER + LAST), 4], BF16, align_bytes=64, name="turn9")
        wg_upper = w_halves[:, 0 : PASSES * UPPER, :].rearrange("p (g n) t -> p g n t", g=PASSES)
        wg_last = w_halves[:, PASSES * UPPER :, :].rearrange("p (g n) t -> p g n t", g=PASSES)
        wc = const.tile([P, PASSES * (UPPER + LAST)], U32, align_bytes=64)
        ws = const.tile([P, PASSES * (UPPER + LAST)], U8, align_bytes=64)

        def regroup_levels_7_8(g):
            nc.vector.tensor_copy(
                out=wg_upper[:, g].rearrange("p (c i) t -> p c t i", i=4),
                in_=w_planes[:, g, :, 127:511].rearrange("p t (c i) -> p c t i", i=4),
            )

        def regroup_level_9(copy, g):
            sides_out = wg_last[:, g].rearrange("p (c j i) t -> p c j t i", c=2, i=4)
            sides_in = w_planes[:, g, :, 511:1023].rearrange("p t (j i c) -> p c j t i", c=2, i=4)
            for c in range(2):
                copy(out=sides_out[:, c], in_=sides_in[:, c])

        def quantise_w(first, width):
            nc.vector.quantize_mx(
                out=wc[:, first : first + width].bitcast(FP8X4),
                scales=ws[:, first : first + width],
                in_=w_halves[:, first : first + width, :].rearrange("p n t -> p (n t)"),
            )

        def w_first(slot, g):
            if slot < 3:
                return UPPER * g + P * slot
            return PASSES * UPPER + LAST * g + P * (slot - 3)

        xg_of = {}
        xq_of = {}

        def x_transpose(n, h, g):
            if not live(n):
                return
            if h == 0 and g == 0:
                xg_of[n] = work.tile([P, PASSES, CHUNK, 4], BF16, align_bytes=64, name="xg")
            xt = psum_stream.tile([P, 2, HALF], F32, name="stream")
            for u in range(2):
                for qq in range(2):
                    first = 256 * g + 128 * u
                    nc.tensor.transpose(
                        out=xt[:, u, P * qq : P * qq + P],
                        in_=x_rows[n][:, 2 * h + qq, :].bitcast(F32)[:, first : first + P],
                        identity=ident[:],
                    )
            dst = xg_of[n][:, g, HALF * h : HALF * h + HALF, :].rearrange("p b t -> p (b t)").bitcast(F32)
            nc.scalar.copy(out=dst.rearrange("p (b u) -> p b u", u=2), in_=xt[:].rearrange("p u b -> p b u"))

        def x_quantise(n):
            if not live(n):
                return
            xc = xqp.tile([P, PASSES, CHUNK], U32, align_bytes=64)
            xs = xqp.tile([P, PASSES, CHUNK], U8, align_bytes=64)
            xq_of[n] = (xc, xs)
            nc.vector.quantize_mx(
                out=xc[:].rearrange("p g b -> p (g b)").bitcast(FP8X4),
                scales=xs[:].rearrange("p g b -> p (g b)"),
                in_=xg_of[n][:].rearrange("p g b t -> p (g b t)"),
            )

        turn_of = {}

        top_of = {}

        def top_logits(n, q):
            if not live(n):
                return
            if q == 0:
                top_of[n] = psum_top.tile([P, ROW_TILES, TOP], F32, name="top")
            for g in range(PASSES):
                for t in range(4):
                    nc.tensor.matmul(
                        out=top_of[n][:, q, :],
                        lhsT=xg_of[n][:, g, P * q : P * q + P, t],
                        rhs=top_planes[:, g, t, :],
                        start=(g == 0 and t == 0),
                        stop=False,
                    )
            nc.tensor.matmul(out=top_of[n][:, q, :], lhsT=ones[:], rhs=bias_row[:], start=False, stop=True)

        def top_turns(n):
            if not live(n):
                return
            turn = work.tile([P, 2, ROW_TILES, TOP], F32, name="turn")
            for c, scale in ((1, 1.0), (0, -1.0)):
                nc.scalar.activation(out=turn[:, c], in_=top_of[n][:], func=SIGMOID, scale=scale)
            turn_of[n] = turn

        reach_of = {}

        def sweep_level(n, level):
            if not live(n):
                return
            turn = turn_of[n]
            nodes = 2**level
            if level == 1:
                reach = turn[:, :, :, 0].rearrange("p c q -> p q c")
            else:
                reach = reach_of[n][:]
            children = work.tile([P, ROW_TILES, 2 * nodes], F32, name="reach%d" % (level + 1))
            nc.vector.tensor_tensor(
                out=children[:].rearrange("p q (j c) -> p q j c", c=2),
                in0=reach.unsqueeze(3).to_broadcast([P, ROW_TILES, nodes, 2]),
                in1=turn[:, :, :, nodes - 1 : 2 * nodes - 1].rearrange("p c q j -> p q j c"),
                op=ALU.mult,
            )
            reach_of[n] = children

        low_of = {}
        pt_of = {}

        def low_logits(xc, xs, slot):
            z = psum_stream.tile([P, CHUNK], F32, name="stream")
            for g in range(PASSES):
                nc.tensor.matmul_mx(
                    out=z[:],
                    lhsT=wc[:, w_first(slot, g) : w_first(slot, g) + P].bitcast(FP8X4),
                    lhsT_scale=ws[:, w_first(slot, g) : w_first(slot, g) + P],
                    rhs=xc[:, g, :].bitcast(FP8X4),
                    rhs_scale=xs[:, g, :],
                    start=(g == 0),
                    stop=(g == PASSES - 1),
                )
            return z

        logits7_of = {}

        def low_turn(n, slot):
            if not live(n):
                return
            pieces = pieces_of(n)
            width = CHUNK // pieces
            if slot == 0:
                logits7_of[n] = work.tile([P, CHUNK], F32, name="logits7")
            elif n not in low_of:
                right8 = work.tile([P, pieces, 2, width], F32)
                turn9 = turns.tile([P, pieces, 2, 2, 2, width], F32, align_bytes=64, name="turn9")
                low_of[n] = (None, right8, turn9)
            right8, turn9 = low_of[n][1:] if slot > 0 else (None, None)
            z = low_logits(xq_of[n][0], xq_of[n][1], slot)
            z_pieces = z[:].rearrange("p (h b) -> p h b", h=pieces)
            if slot == 0:
                nc.scalar.activation(out=logits7_of[n][:], in_=z[:], func=IDENTITY, bias=column(64))
            elif slot < 3:
                nc.scalar.activation(
                    out=right8[:, :, slot - 1, :], in_=z_pieces, func=SIGMOID, bias=column(32 + slot - 1)
                )
            else:
                i = slot - 3
                c, g9 = divmod(i, 2)
                nc.scalar.activation(out=turn9[:, :, c, 1, g9, :], in_=z_pieces, func=SIGMOID, bias=column(i))

        def turn7_transpose(n):
            if not live(n):
                return
            pt = psum_stream.tile([P, ROW_TILES, P], F32, name="stream")
            for q in range(ROW_TILES):
                nc.tensor.transpose(
                    out=pt[:, q, :], in_=logits7_of[n][:, P * q : P * q + P], identity=ident[:]
                )
            turn7 = work.tile([P, 2, ROW_TILES, P], F32, name="turn7")
            for c, scale in ((1, 1.0), (0, -1.0)):
                nc.scalar.activation(out=turn7[:, c], in_=pt[:], func=SIGMOID, scale=scale)
            turn7_of[n] = turn7

        turn7_of = {}
        reach8_of = {}
        reach9_of = {}
        probs_of = {}
        pq_of = {}

        def sweep_level_7(n):
            if not live(n):
                return
            reach8_of[n] = work.tile([P, ROW_TILES, 256], F32, name="reach8")
            nc.vector.tensor_tensor(
                out=reach8_of[n][:].rearrange("p q (j c) -> p (q j) c", c=2),
                in0=reach_of[n][:].rearrange("p q j -> p (q j)").unsqueeze(2).to_broadcast([P, ROW_TILES * P, 2]),
                in1=turn7_of[n][:].rearrange("p c q j -> p (q j) c"),
                op=ALU.mult,
            )

        def reach8_transpose(n):
            if not live(n):
                return
            banks = []
            for g in range(2):
                pt = psum_pt.tile([P, CHUNK], F32, name="pt")
                for q in range(ROW_TILES):
                    nc.tensor.transpose(
                        out=pt[:, P * q : P * q + P],
                        in_=reach8_of[n][:, q, P * g : P * g + P],
                        identity=ident[:],
                    )
                banks.append(pt)
            pt_of[n] = banks

        def reach9(n, c, g):
            if not live(n):
                return
            pieces = pieces_of(n)
            if c == 1 and g == 0:
                reach9_of[n] = work.tile(
                    [P, pieces, 2, CHUNK // pieces // 4, 2, 4], F32, align_bytes=64, name="reach9"
                )
            parent = pt_of[n][g][:].rearrange("p (h k i) -> p h k i", h=pieces, i=4)
            right = reach9_of[n][:, :, g, :, 1, :]
            if c == 1:
                turn = low_of[n][1][:, :, g, :].rearrange("p h (k i) -> p h k i", i=4)
                nc.vector.tensor_tensor(out=right, in0=parent, in1=turn, op=ALU.mult)
            else:
                nc.vector.tensor_tensor(out=reach9_of[n][:, :, g, :, 0, :], in0=parent, in1=right, op=ALU.subtract)

        def turn9_left(n):
            if not live(n):
                return
            minus = work.tile([P, 1], F32, name="minus")
            nc.vector.memset(minus[:], -1.0)
            turn9 = low_of[n][2]
            nc.gpsimd.tensor_scalar(
                out=turn9[:, :, 1, 0].rearrange("p h g b -> p h (g b)"),
                in0=turn9[:, :, 1, 1].rearrange("p h g b -> p h (g b)"),
                scalar1=minus[:], scalar2=1.0, op0=ALU.mult, op1=ALU.add,
            )
            nc.gpsimd.tensor_scalar(
                out=turn9[:, :, 0, 0, 0], in0=turn9[:, :, 0, 1, 0],
                scalar1=minus[:], scalar2=1.0, op0=ALU.mult, op1=ALU.add,
            )

        def turn9_v(n):
            if not live(n):
                return
            turn9 = low_of[n][2]
            nc.vector.tensor_scalar(
                out=turn9[:, :, 0, 0, 1], in0=turn9[:, :, 0, 1, 1],
                scalar1=-1.0, scalar2=1.0, op0=ALU.mult, op1=ALU.add,
            )

        def leaf_probs(n, h):
            if not live(n):
                return
            pieces = pieces_of(n)
            width = CHUNK // pieces
            if h == 0:
                probs_of[n] = work.tile([P, pieces, PASSES, width, 4], BF16, align_bytes=64, name="probs")
                pc = work.tile([P, pieces, PASSES, width], U32, align_bytes=64)
                ps = work.tile([P, pieces, PASSES, width], U8, align_bytes=64)
                pq_of[n] = (pc, ps)
            fours = PASSES * width // 4
            parent = reach9_of[n][:, h].rearrange("p g k c i -> p (g k) c i")
            turn = low_of[n][2][:, h].rearrange("p c e g b -> p c e (g b)")
            leaf = probs_of[n][:, h].rearrange("p g b t -> p (g b) t")
            nc.vector.tensor_tensor(
                out=leaf.rearrange("p (k i) (c e) -> p k c e i", i=4, e=2),
                in0=parent.unsqueeze(3).to_broadcast([P, fours, 2, 2, 4]),
                in1=turn.rearrange("p c e (k i) -> p k c e i", i=4),
                op=ALU.mult,
            )

        def leaf_quantise(n, h):
            if not live(n):
                return
            pc, ps = pq_of[n]
            nc.vector.quantize_mx(
                out=pc[:, h].rearrange("p g b -> p (g b)").bitcast(FP8X4),
                scales=ps[:, h].rearrange("p g b -> p (g b)"),
                in_=probs_of[n][:, h].rearrange("p g b t -> p (g b t)"),
            )

        rows_of = {}

        def leaves(n, q, half):
            if not live(n):
                return
            pc, ps = pq_of[n]
            h, first = divmod(P * q, CHUNK // pieces_of(n))
            if half == 0:
                rows_of[n] = ostage.tile([P, CLASSES], F32, name="rows")
            acc = psum_stream.tile([P, 512], F32, name="stream")
            for g in range(PASSES):
                nc.tensor.matmul_mx(
                    out=acc[:],
                    lhsT=pc[:, h, g, first : first + P].bitcast(FP8X4),
                    lhsT_scale=ps[:, h, g, first : first + P],
                    rhs=leaf_words[:, g, 2048 * half : 2048 * half + 2048].bitcast(FP8X4),
                    rhs_scale=leaf_scales[:, g, 512 * half : 512 * half + 512],
                    start=(g == 0),
                    stop=(g == PASSES - 1),
                )
            last = n == CHUNKS - 1 and q == ROW_TILES - 1
            cols = slice(512 * half, 512 * half + 512)
            copy = nc.vector.tensor_copy if last and half == 1 else nc.scalar.copy
            copy(out=rows_of[n][:, cols], in_=acc[:])
            if last:
                nc.sync.dma_start(out=out_tiles[n, q][:, cols], in_=rows_of[n][:, cols])
            elif half == 1:
                nc.sync.dma_start(out=out_tiles[n, q], in_=rows_of[n][:])

        def top(n):
            for q in range(ROW_TILES):
                top_logits(n, q)
            top_turns(n)

        def x_in(n):
            for q in range(ROW_TILES):
                x_transpose(n, q // 2, q % 2)

        def period(f):
            x_in(f)
            turn7_transpose(f - 1)
            reach9(f - 2, 0, 0)
            reach9(f - 2, 0, 1)
            turn9_v(f - 2)
            sweep_level(f - 1, 4)
            if f - 3 != CHUNKS - 1:
                leaf_quantise(f - 3, 1)
            leaves(f - 3, 0, 0)
            low_turn(f - 1, 5)
            leaves(f - 3, 0, 1)
            leaves(f - 3, 1, 0)
            sweep_level(f - 1, 5)
            leaf_probs(f - 2, 0)
            if f - 2 == CHUNKS - 1:
                leaf_probs(f - 2, 1)
            sweep_level(f - 1, 6)
            leaf_quantise(f - 2, 0)
            sweep_level_7(f - 1)
            x_quantise(f)
            top(f)
            leaves(f - 3, 1, 1)
            low_turn(f - 1, 1)
            leaves(f - 3, 2, 0)
            low_turn(f - 1, 2)
            sweep_level(f, 1)
            low_turn(f - 1, 6)
            sweep_level(f, 2)
            reach8_transpose(f - 1)
            leaves(f - 3, 2, 1)
            if f - 2 == CHUNKS - 1:
                leaf_probs(f - 2, 2)
                leaf_quantise(f - 2, 1)
                leaf_quantise(f - 2, 2)
                leaf_probs(f - 2, 3)
                leaf_quantise(f - 2, 3)
            else:
                leaf_probs(f - 2, 1)
            low_turn(f - 1, 3)
            low_turn(f - 1, 4)
            sweep_level(f, 3)
            turn9_left(f - 1)
            reach9(f - 1, 1, 0)
            reach9(f - 1, 1, 1)
            low_turn(f, 0)
            for half in range(2):
                leaves(f - 3, 3, half)

        warm_up(3)
        x_in(0)
        spread_bias()
        x_quantise(0)
        top(0)
        warm_up(8)
        regroup_levels_7_8(0)
        regroup_levels_7_8(1)
        regroup_level_9(nc.scalar.copy, 1)
        quantise_w(0, 512)
        regroup_level_9(nc.vector.tensor_copy, 0)
        quantise_w(PASSES * UPPER, PASSES * LAST)
        quantise_w(512, 256)
        for level in range(1, 4):
            sweep_level(0, level)
        low_turn(0, 0)
        for f in range(1, CHUNKS + 3):
            period(f)
